import numpy as np
import ml_dtypes


def mxq(x, axis, fmt="e4m3"):
    dtype, down = {"e4m3": (ml_dtypes.float8_e4m3fn, 7), "e5m2": (ml_dtypes.float8_e5m2, 14)}[fmt]
    v = np.moveaxis(np.asarray(x, np.float32).astype(ml_dtypes.bfloat16).astype(np.float64), axis, -1)
    blocks = v.reshape(v.shape[:-1] + (-1, 32))
    amax = np.abs(blocks).max(-1, keepdims=True)
    byte = np.maximum(np.where(amax > 0, np.frexp(amax)[1] - 1 + 127, 0) - down, 1)
    scale = np.exp2(byte - 127.0)
    codes = (blocks / scale).astype(np.float32).astype(dtype).astype(np.float64)
    return np.moveaxis((codes * scale).reshape(v.shape), -1, axis)


WIDE = False


def mx_kscale(k):
    if not WIDE:
        return np.ones(k)
    levels = np.array([10, -10, 5, -5, 0])
    a = np.random.permutation(np.resize(levels, k // 512 * 4)).reshape(k // 512, 4)
    idx = np.arange(k)
    return np.exp2(a[idx // 512, idx % 128 // 32])


BF16 = ml_dtypes.bfloat16


def bf(x):
    return np.asarray(x, np.float32).astype(BF16)


def f64(x):
    return np.asarray(x).astype(np.float64)


E2M1 = np.array([0.0, 0.5, 1.0, 1.5, 2.0, 3.0, 4.0, 6.0, -0.0, -0.5, -1.0, -1.5, -2.0, -3.0, -4.0, -6.0])


def pack_weight(w, fmt):
    k, n = w.shape
    w = f64(bf(w)).reshape(k // 32, 32, n)
    amax = np.abs(w).max(1)
    if fmt == "e4m3":
        byte = np.frexp(amax)[1] - 1 + 127 - 7
    else:
        mant, ex = np.frexp(amax / 6.0)
        byte = np.where(mant > 0.5, ex, ex - 1) + 127
    byte = np.clip(np.where(amax > 0, byte, 1), 1, 254)
    scaled = (w * np.exp2(127.0 - byte)[:, None, :]).reshape(k, n).astype(np.float32)
    by_word = np.ascontiguousarray(scaled.reshape(k // 512, 128, 4, n).transpose(0, 1, 3, 2))
    if fmt == "e4m3":
        words = by_word.astype(ml_dtypes.float8_e4m3fn).view(np.uint8)
    else:
        c = by_word.astype(ml_dtypes.float4_e2m1fn).view(np.uint8) & 0xF
        words = c[..., 0::2] | (c[..., 1::2] << 4)
    return np.ascontiguousarray(words), np.ascontiguousarray(byte.astype(np.uint8).reshape(k // 512, 16, n))


def unpack_weight(words, scales, fmt):
    g, p, n, _ = words.shape
    if fmt == "e4m3":
        vals = np.ascontiguousarray(words).view(ml_dtypes.float8_e4m3fn).astype(np.float64)
    else:
        nib = np.empty((g, p, n, 4), np.uint8)
        nib[..., 0::2] = words & 0xF
        nib[..., 1::2] = words >> 4
        vals = E2M1[nib]
    vals = vals * np.repeat(np.exp2(scales.astype(np.float64) - 127.0), 8, axis=1)[..., None]
    return vals.transpose(0, 1, 3, 2).reshape(g * 512, n)


B, S, E, H, D, XL, TOPK = 2, 256, 1024, 8, 128, 512, 8
HD = H * D
FMT = "e4m3"


def l2norm(x):
    return x / np.maximum(np.sqrt((x * x).sum(-1, keepdims=True)), 1e-12)


def split_heads(x):
    return x.reshape(B, S, H, D).transpose(0, 2, 1, 3)


def setup_inputs():
    n = np.random.standard_normal
    s = mx_kscale(E)
    x = bf(n((B, S, E)) * s)
    Wq_words, Wq_scales = pack_weight((n((HD, E)) / np.sqrt(E) / s).T, FMT)
    bq = bf(n(HD) * 0.1)
    Wk_words, Wk_scales = pack_weight((n((HD, E)) / np.sqrt(E) / s).T, FMT)
    bk = bf(n(HD) * 0.1)
    Wv_words, Wv_scales = pack_weight((n((HD, E)) / np.sqrt(E) / s).T, FMT)
    bv = bf(n(HD) * 0.1)
    return {"input": x,
            "Wq_words": Wq_words, "Wq_scales": Wq_scales, "bq": bq,
            "Wk_words": Wk_words, "Wk_scales": Wk_scales, "bk": bk,
            "Wv_words": Wv_words, "Wv_scales": Wv_scales, "bv": bv}


def reference(input, Wq_words, Wq_scales, bq, Wk_words, Wk_scales, bk, Wv_words, Wv_scales, bv):
    xq = mxq(f64(input), 2, "e4m3")
    q = split_heads(l2norm((xq @ unpack_weight(Wq_words, Wq_scales, FMT)) + f64(bq)))
    k = split_heads(l2norm((xq @ unpack_weight(Wk_words, Wk_scales, FMT)) + f64(bk)))
    v = split_heads((xq @ unpack_weight(Wv_words, Wv_scales, FMT)) + f64(bv))
    return q, k, v

@@ -1,0 +1,189 @@
+from contextlib import ExitStack
+
+import concourse.mybir as mybir
+from concourse.masks import make_identity
+
+F32 = mybir.dt.float32
+BF16 = mybir.dt.bfloat16
+I32 = mybir.dt.int32
+U32 = mybir.dt.uint32
+U8 = mybir.dt.uint8
+FP8X4 = mybir.dt.float8_e4m3fn_x4
+ALU = mybir.AluOpType
+ACT = mybir.ActivationFunctionType
+
+P = 128
+BATCH = 2
+SEQ = 256
+EMBED = 1024
+FEATURES = 1024
+HEADS = 8
+HEAD_DIM = 128
+TOKEN_TILES = BATCH * SEQ // P
+K_PASS = 4 * P
+PASSES = EMBED // K_PASS
+BANK = 512
+BANKS_PER_ROW = FEATURES // BANK
+HEADS_PER_BANK = BANK // HEAD_DIM
+WORDS_PER_PASS = K_PASS // 2
+SCALE_ROWS = 4
+QUADRANTS = 4
+
+FLOPS = 2 * BATCH * SEQ * EMBED * 3 * FEATURES
+
+
+def tile_knnxlmultiheadsattention_pa_kernel(
+    tc,
+    x,
+    wq_words,
+    wq_scales,
+    bq,
+    wk_words,
+    wk_scales,
+    bk,
+    wv_words,
+    wv_scales,
+    bv,
+    out_q,
+    out_k,
+    out_v,
+):
+    nc = tc.nc
+    projections = [
+        dict(name="v", words=wv_words, scales=wv_scales, bias=bv, out=out_v, normalise=False),
+        dict(name="q", words=wq_words, scales=wq_scales, bias=bq, out=out_q, normalise=True),
+        dict(name="k", words=wk_words, scales=wk_scales, bias=bk, out=out_k, normalise=True),
+    ]
+    count = len(projections)
+
+    with ExitStack() as stack:
+        keep = stack.enter_context(tc.tile_pool(name="keep", bufs=1))
+        small = stack.enter_context(tc.tile_pool(name="small", bufs=4))
+        psum = stack.enter_context(tc.psum_pool(name="psum", bufs=8))
+
+        x_sb = keep.tile([P, TOKEN_TILES, EMBED], BF16)
+        x_codes = keep.tile([P, TOKEN_TILES, PASSES * P], U32, align_bytes=64)
+        x_scales = keep.tile([P, TOKEN_TILES, PASSES * P], U8, align_bytes=64)
+        w_codes = keep.tile([P, count, PASSES, FEATURES], I32, align_bytes=64)
+        w_scales = keep.tile([P, count, FEATURES], U8, align_bytes=64)
+        bias_rows = keep.tile([P, count, FEATURES], BF16)
+        bias_all = keep.tile([P, count, FEATURES], F32)
+        ones = keep.tile([P, P], BF16)
+        identity = keep.tile([P, P], F32)
+        minus_half = keep.tile([P, 1], F32)
+
+        nc.vector.memset(w_scales[:].bitcast(I32), 0)
+        nc.vector.memset(bias_rows[:], 0.0)
+        nc.vector.memset(ones[:], 1.0)
+        nc.vector.memset(minus_half[:], -0.5)
+        make_identity(nc, identity[:])
+
+        x_by_tile = x.rearrange("b (c j) e -> j c b e", j=TOKEN_TILES)
+        for j in range(TOKEN_TILES):
+            nc.sync.dma_start(out=x_sb[:, j, :], in_=x_by_tile[j])
+        for i, proj in enumerate(projections):
+            for quadrant in range(QUADRANTS):
+                first = 32 * quadrant
+                rows = slice(SCALE_ROWS * quadrant, SCALE_ROWS * (quadrant + 1))
+                nc.sync.dma_start(
+                    out=w_scales[first : first + PASSES * SCALE_ROWS, i, :].bitcast(I32),
+                    in_=proj["scales"][:, rows, :].bitcast(I32),
+                )
+            for g in range(PASSES):
+                nc.sync.dma_start(
+                    out=w_codes[:, i, g, :],
+                    in_=proj["words"][g].rearrange("p n t -> p (n t)").bitcast(I32),
+                )
+            nc.gpsimd.dma_start(
+                out=bias_rows[0:1, i, :], in_=proj["bias"].rearrange("(o n) -> o n", o=1)
+            )
+
+        for i in range(count):
+            for nb in range(BANKS_PER_ROW):
+                cols = slice(BANK * nb, BANK * (nb + 1))
+                spread = psum.tile([P, BANK], F32, tag="bank")
+                nc.tensor.matmul(
+                    out=spread[:], lhsT=ones[:], rhs=bias_rows[:, i, cols], start=True, stop=True
+                )
+                nc.scalar.copy(out=bias_all[:, i, cols], in_=spread[:])
+
+        x_words = x_sb[:].bitcast(F32)
+        for j in range(TOKEN_TILES):
+            flipped = psum.tile([P, PASSES, 2, P], F32, tag="bank")
+            for g in range(PASSES):
+                for u in range(2):
+                    nc.tensor.transpose(
+                        flipped[:, g, u, :],
+                        x_words[:, j, WORDS_PER_PASS * g + u : WORDS_PER_PASS * (g + 1) : 2],
+                        identity[:],
+                    )
+            grouped = keep.tile([P, PASSES * P * 4], BF16, align_bytes=64, name="grouped%d" % j)
+            grouped_words = grouped[:].bitcast(F32).rearrange("p (g r u) -> p g r u", g=PASSES, u=2)
+            if j % 2 == 0:
+                nc.vector.tensor_copy(out=grouped_words, in_=flipped[:].rearrange("p g u r -> p g r u"))
+            else:
+                nc.scalar.copy(out=grouped_words, in_=flipped[:].rearrange("p g u r -> p g r u"))
+            nc.vector.quantize_mx(
+                out=x_codes[:, j, :].bitcast(FP8X4), scales=x_scales[:, j, :], in_=grouped[:]
+            )
+
+        for i, proj in enumerate(projections):
+            y = keep.tile([P, HEADS, TOKEN_TILES, HEAD_DIM], F32, name="y_" + proj["name"])
+            for j in range(TOKEN_TILES):
+                sums = small.tile([P, BANKS_PER_ROW], F32)
+                for nb in range(BANKS_PER_ROW):
+                    cols = slice(BANK * nb, BANK * (nb + 1))
+                    heads = slice(HEADS_PER_BANK * nb, HEADS_PER_BANK * (nb + 1))
+                    acc = psum.tile([P, BANK], F32, tag="bank")
+                    for g in range(PASSES):
+                        tokens = slice(P * g, P * (g + 1))
+                        nc.tensor.matmul_mx(
+                            out=acc[:],
+                            lhsT=x_codes[:, j, tokens].bitcast(FP8X4),
+                            lhsT_scale=x_scales[:, j, tokens],
+                            rhs=w_codes[:, i, g, cols].bitcast(FP8X4),
+                            rhs_scale=w_scales[SCALE_ROWS * g : P, i, cols],
+                            start=(g == 0),
+                            stop=(g == PASSES - 1),
+                        )
+                    nc.vector.tensor_tensor(
+                        out=y[:, heads, j, :],
+                        in0=acc[:].rearrange("p (h d) -> p h d", d=HEAD_DIM),
+                        in1=bias_all[:, i, cols].rearrange("p (h d) -> p h d", d=HEAD_DIM),
+                        op=ALU.add,
+                    )
+                    if proj["normalise"]:
+                        squares = small.tile([P, HEADS_PER_BANK, HEAD_DIM], F32)
+                        nc.scalar.activation(
+                            out=squares[:],
+                            in_=y[:, heads, j, :],
+                            func=ACT.Square,
+                            accum_out=sums[:, nb : nb + 1],
+                        )
+                if proj["normalise"]:
+                    floored = small.tile([P, 1], F32)
+                    nc.gpsimd.tensor_scalar(
+                        out=floored[:],
+                        in0=sums[:, 0:1],
+                        scalar1=sums[:, 1:2],
+                        scalar2=1e-24,
+                        op0=ALU.add,
+                        op1=ALU.max,
+                    )
+                    inverse = small.tile([P, 1], F32)
+                    nc.gpsimd.tensor_tensor(
+                        out=inverse[:], in0=floored[:], in1=minus_half[:], op=ALU.pow
+                    )
+                    nc.gpsimd.tensor_scalar(
+                        out=y[:, :, j, :],
+                        in0=y[:, :, j, :],
+                        scalar1=inverse[:, 0:1],
+                        scalar2=0.0,
+                        op0=ALU.mult,
+                        op1=ALU.add,
+                    )
+            out_by_head = proj["out"].rearrange("b h (c j) d -> h c b (j d)", j=TOKEN_TILES)
+            for h in range(HEADS):
+                nc.sync.dma_start(
+                    out=out_by_head[h], in_=y[:, h, :, :].rearrange("p j d -> p (j d)")
+                )

@@ -28,6 +28,8 @@ HEADS_PER_BANK = BANK // HEAD_DIM
 WORDS_PER_PASS = K_PASS // 2
 SCALE_ROWS = 4
 QUADRANTS = 4
+STORE_TILES = 2
+NORM_FLOOR_SQUARED = 1e-24
 
 FLOPS = 2 * BATCH * SEQ * EMBED * 3 * FEATURES
 
@@ -70,17 +72,22 @@ def tile_knnxlmultiheadsattention_pa_kernel(
         bias_all = keep.tile([P, count, FEATURES], F32)
         ones = keep.tile([P, P], BF16)
         identity = keep.tile([P, P], F32)
-        minus_half = keep.tile([P, 1], F32)
+        one = keep.tile([P, 1], F32)
+        table_warmer = keep.tile([P, 1], F32)
 
         nc.vector.memset(w_scales[:].bitcast(I32), 0)
+        nc.vector.memset(one[:], 1.0)
         nc.vector.memset(bias_rows[:], 0.0)
         nc.vector.memset(ones[:], 1.0)
-        nc.vector.memset(minus_half[:], -0.5)
         make_identity(nc, identity[:])
+        nc.scalar.activation(out=table_warmer[:], in_=one[:], func=ACT.Abs_reciprocal_sqrt)
 
-        x_by_tile = x.rearrange("b (c j) e -> j c b e", j=TOKEN_TILES)
-        for j in range(TOKEN_TILES):
-            nc.sync.dma_start(out=x_sb[:, j, :], in_=x_by_tile[j])
+        x_by_half = x.rearrange("b (c half je) e -> half c b (je e)", half=2, je=TOKEN_TILES // 2)
+        for half in range(2):
+            tiles = slice(TOKEN_TILES // 2 * half, TOKEN_TILES // 2 * (half + 1))
+            nc.sync.dma_start(
+                out=x_sb[:, tiles, :].rearrange("p j e -> p (j e)"), in_=x_by_half[half]
+            )
         for i, proj in enumerate(projections):
             for quadrant in range(QUADRANTS):
                 first = 32 * quadrant
@@ -98,15 +105,6 @@ def tile_knnxlmultiheadsattention_pa_kernel(
                 out=bias_rows[0:1, i, :], in_=proj["bias"].rearrange("(o n) -> o n", o=1)
             )
 
-        for i in range(count):
-            for nb in range(BANKS_PER_ROW):
-                cols = slice(BANK * nb, BANK * (nb + 1))
-                spread = psum.tile([P, BANK], F32, tag="bank")
-                nc.tensor.matmul(
-                    out=spread[:], lhsT=ones[:], rhs=bias_rows[:, i, cols], start=True, stop=True
-                )
-                nc.scalar.copy(out=bias_all[:, i, cols], in_=spread[:])
-
         x_words = x_sb[:].bitcast(F32)
         for j in range(TOKEN_TILES):
             flipped = psum.tile([P, PASSES, 2, P], F32, tag="bank")
@@ -119,26 +117,35 @@ def tile_knnxlmultiheadsattention_pa_kernel(
                     )
             grouped = keep.tile([P, PASSES * P * 4], BF16, align_bytes=64, name="grouped%d" % j)
             grouped_words = grouped[:].bitcast(F32).rearrange("p (g r u) -> p g r u", g=PASSES, u=2)
-            if j % 2 == 0:
-                nc.vector.tensor_copy(out=grouped_words, in_=flipped[:].rearrange("p g u r -> p g r u"))
-            else:
-                nc.scalar.copy(out=grouped_words, in_=flipped[:].rearrange("p g u r -> p g r u"))
+            nc.scalar.copy(out=grouped_words, in_=flipped[:].rearrange("p g u r -> p g r u"))
             nc.vector.quantize_mx(
                 out=x_codes[:, j, :].bitcast(FP8X4), scales=x_scales[:, j, :], in_=grouped[:]
             )
 
         for i, proj in enumerate(projections):
+            for nb in range(BANKS_PER_ROW):
+                cols = slice(BANK * nb, BANK * (nb + 1))
+                spread = psum.tile([P, BANK], F32, tag="bank")
+                nc.tensor.matmul(
+                    out=spread[:], lhsT=ones[:], rhs=bias_rows[:, i, cols], start=True, stop=True
+                )
+                nc.scalar.copy(out=bias_all[:, i, cols], in_=spread[:])
+
             y = keep.tile([P, HEADS, TOKEN_TILES, HEAD_DIM], F32, name="y_" + proj["name"])
+            out_runs = proj["out"].rearrange(
+                "b h (c r j) d -> r h c b (j d)", r=TOKEN_TILES // STORE_TILES, j=STORE_TILES
+            )
             for j in range(TOKEN_TILES):
-                sums = small.tile([P, BANKS_PER_ROW], F32)
-                for nb in range(BANKS_PER_ROW):
-                    cols = slice(BANK * nb, BANK * (nb + 1))
-                    heads = slice(HEADS_PER_BANK * nb, HEADS_PER_BANK * (nb + 1))
-                    acc = psum.tile([P, BANK], F32, tag="bank")
-                    for g in range(PASSES):
-                        tokens = slice(P * g, P * (g + 1))
+                accs = [
+                    psum.tile([P, BANK], F32, tag="bank", name="acc%d" % nb)
+                    for nb in range(BANKS_PER_ROW)
+                ]
+                for g in range(PASSES):
+                    tokens = slice(P * g, P * (g + 1))
+                    for nb in range(BANKS_PER_ROW):
+                        cols = slice(BANK * nb, BANK * (nb + 1))
                         nc.tensor.matmul_mx(
-                            out=acc[:],
+                            out=accs[nb][:],
                             lhsT=x_codes[:, j, tokens].bitcast(FP8X4),
                             lhsT_scale=x_scales[:, j, tokens],
                             rhs=w_codes[:, i, g, cols].bitcast(FP8X4),
@@ -146,44 +153,43 @@ def tile_knnxlmultiheadsattention_pa_kernel(
                             start=(g == 0),
                             stop=(g == PASSES - 1),
                         )
+                for nb in range(BANKS_PER_ROW):
+                    cols = slice(BANK * nb, BANK * (nb + 1))
+                    heads = slice(HEADS_PER_BANK * nb, HEADS_PER_BANK * (nb + 1))
                     nc.vector.tensor_tensor(
                         out=y[:, heads, j, :],
-                        in0=acc[:].rearrange("p (h d) -> p h d", d=HEAD_DIM),
+                        in0=accs[nb][:].rearrange("p (h d) -> p h d", d=HEAD_DIM),
                         in1=bias_all[:, i, cols].rearrange("p (h d) -> p h d", d=HEAD_DIM),
                         op=ALU.add,
                     )
-                    if proj["normalise"]:
-                        squares = small.tile([P, HEADS_PER_BANK, HEAD_DIM], F32)
-                        nc.scalar.activation(
-                            out=squares[:],
-                            in_=y[:, heads, j, :],
-                            func=ACT.Square,
-                            accum_out=sums[:, nb : nb + 1],
-                        )
                 if proj["normalise"]:
-                    floored = small.tile([P, 1], F32)
-                    nc.gpsimd.tensor_scalar(
-                        out=floored[:],
-                        in0=sums[:, 0:1],
-                        scalar1=sums[:, 1:2],
-                        scalar2=1e-24,
-                        op0=ALU.add,
-                        op1=ALU.max,
+                    squares = small.tile([P, HEADS, HEAD_DIM], F32)
+                    sum_squares = small.tile([P, 1], F32)
+                    nc.scalar.activation(
+                        out=squares[:], in_=y[:, :, j, :], func=ACT.Square, accum_out=sum_squares[:]
                     )
-                    inverse = small.tile([P, 1], F32)
-                    nc.gpsimd.tensor_tensor(
-                        out=inverse[:], in0=floored[:], in1=minus_half[:], op=ALU.pow
+                    above_floor = small.tile([P, 1], F32)
+                    nc.scalar.activation(
+                        out=above_floor[:], in_=sum_squares[:], func=ACT.Relu, bias=-NORM_FLOOR_SQUARED
                     )
-                    nc.gpsimd.tensor_scalar(
+                    inverse_norm = small.tile([P, 1], F32)
+                    nc.scalar.activation(
+                        out=inverse_norm[:],
+                        in_=above_floor[:],
+                        func=ACT.Abs_reciprocal_sqrt,
+                        bias=NORM_FLOOR_SQUARED,
+                    )
+                    nc.vector.tensor_scalar(
                         out=y[:, :, j, :],
                         in0=y[:, :, j, :],
-                        scalar1=inverse[:, 0:1],
-                        scalar2=0.0,
+                        scalar1=inverse_norm[:, 0:1],
+                        scalar2=None,
                         op0=ALU.mult,
-                        op1=ALU.add,
                     )
-            out_by_head = proj["out"].rearrange("b h (c j) d -> h c b (j d)", j=TOKEN_TILES)
-            for h in range(HEADS):
-                nc.sync.dma_start(
-                    out=out_by_head[h], in_=y[:, h, :, :].rearrange("p j d -> p (j d)")
-                )
+                if (j + 1) % STORE_TILES == 0:
+                    done = slice(j + 1 - STORE_TILES, j + 1)
+                    for h in range(HEADS):
+                        nc.sync.dma_start(
+                            out=out_runs[j // STORE_TILES, h],
+                            in_=y[:, h, done, :].rearrange("p j d -> p (j d)"),
+                        )

@@ -29,6 +29,7 @@ WORDS_PER_PASS = K_PASS // 2
 SCALE_ROWS = 4
 QUADRANTS = 4
 STORE_TILES = 2
+NORM_LAG = 3
 NORM_FLOOR_SQUARED = 1e-24
 
 FLOPS = 2 * BATCH * SEQ * EMBED * 3 * FEATURES
@@ -52,9 +53,9 @@ def tile_knnxlmultiheadsattention_pa_kernel(
 ):
     nc = tc.nc
     projections = [
-        dict(name="v", words=wv_words, scales=wv_scales, bias=bv, out=out_v, normalise=False),
         dict(name="q", words=wq_words, scales=wq_scales, bias=bq, out=out_q, normalise=True),
         dict(name="k", words=wk_words, scales=wk_scales, bias=bk, out=out_k, normalise=True),
+        dict(name="v", words=wv_words, scales=wv_scales, bias=bv, out=out_v, normalise=False),
     ]
     count = len(projections)
 
@@ -62,33 +63,41 @@ def tile_knnxlmultiheadsattention_pa_kernel(
         keep = stack.enter_context(tc.tile_pool(name="keep", bufs=1))
         small = stack.enter_context(tc.tile_pool(name="small", bufs=4))
         psum = stack.enter_context(tc.psum_pool(name="psum", bufs=8))
+        stack.enter_context(tc.manual_schedule())
 
         x_sb = keep.tile([P, TOKEN_TILES, EMBED], BF16)
+        x_grouped = keep.tile([P, TOKEN_TILES, PASSES * P * 4], BF16, align_bytes=64)
         x_codes = keep.tile([P, TOKEN_TILES, PASSES * P], U32, align_bytes=64)
         x_scales = keep.tile([P, TOKEN_TILES, PASSES * P], U8, align_bytes=64)
         w_codes = keep.tile([P, count, PASSES, FEATURES], I32, align_bytes=64)
         w_scales = keep.tile([P, count, FEATURES], U8, align_bytes=64)
         bias_rows = keep.tile([P, count, FEATURES], BF16)
-        bias_all = keep.tile([P, count, FEATURES], F32)
+        bias_all = keep.tile([P, count, FEATURES], BF16)
+        y_all = keep.tile([P, count, HEADS, TOKEN_TILES, HEAD_DIM], F32)
         ones = keep.tile([P, P], BF16)
         identity = keep.tile([P, P], F32)
-        one = keep.tile([P, 1], F32)
-        table_warmer = keep.tile([P, 1], F32)
+        table_warmer = keep.tile([P, 2], F32)
 
+        nc.vector.memset(bias_rows[:].bitcast(I32), 0)
         nc.vector.memset(w_scales[:].bitcast(I32), 0)
-        nc.vector.memset(one[:], 1.0)
-        nc.vector.memset(bias_rows[:], 0.0)
+        nc.vector.memset(table_warmer[:], 1.0)
         nc.vector.memset(ones[:], 1.0)
         make_identity(nc, identity[:])
-        nc.scalar.activation(out=table_warmer[:], in_=one[:], func=ACT.Abs_reciprocal_sqrt)
+        nc.scalar.activation(
+            out=table_warmer[:, 1:2], in_=table_warmer[:, 0:1], func=ACT.Abs_reciprocal_sqrt
+        )
 
-        x_by_half = x.rearrange("b (c half je) e -> half c b (je e)", half=2, je=TOKEN_TILES // 2)
-        for half in range(2):
-            tiles = slice(TOKEN_TILES // 2 * half, TOKEN_TILES // 2 * (half + 1))
-            nc.sync.dma_start(
-                out=x_sb[:, tiles, :].rearrange("p j e -> p (j e)"), in_=x_by_half[half]
-            )
+        half_tiles = TOKEN_TILES // 2
+        x_by_half = x.rearrange("b (c half je) e -> half c b (je e)", half=2, je=half_tiles)
         for i, proj in enumerate(projections):
+            if i < 2:
+                nc.sync.dma_start(
+                    out=x_sb[:, half_tiles * i : half_tiles * (i + 1), :].rearrange("p j e -> p (j e)"),
+                    in_=x_by_half[i],
+                )
+            nc.sync.dma_start(
+                out=bias_rows[0:1, i, :], in_=proj["bias"].rearrange("(o n) -> o n", o=1)
+            )
             for quadrant in range(QUADRANTS):
                 first = 32 * quadrant
                 rows = slice(SCALE_ROWS * quadrant, SCALE_ROWS * (quadrant + 1))
@@ -101,12 +110,10 @@ def tile_knnxlmultiheadsattention_pa_kernel(
                     out=w_codes[:, i, g, :],
                     in_=proj["words"][g].rearrange("p n t -> p (n t)").bitcast(I32),
                 )
-            nc.gpsimd.dma_start(
-                out=bias_rows[0:1, i, :], in_=proj["bias"].rearrange("(o n) -> o n", o=1)
-            )
 
         x_words = x_sb[:].bitcast(F32)
-        for j in range(TOKEN_TILES):
+
+        def quantise_x(j):
             flipped = psum.tile([P, PASSES, 2, P], F32, tag="bank")
             for g in range(PASSES):
                 for u in range(2):
@@ -115,81 +122,102 @@ def tile_knnxlmultiheadsattention_pa_kernel(
                         x_words[:, j, WORDS_PER_PASS * g + u : WORDS_PER_PASS * (g + 1) : 2],
                         identity[:],
                     )
-            grouped = keep.tile([P, PASSES * P * 4], BF16, align_bytes=64, name="grouped%d" % j)
-            grouped_words = grouped[:].bitcast(F32).rearrange("p (g r u) -> p g r u", g=PASSES, u=2)
-            nc.scalar.copy(out=grouped_words, in_=flipped[:].rearrange("p g u r -> p g r u"))
+            nc.vector.tensor_copy(
+                out=x_grouped[:, j, :].bitcast(F32).rearrange("p (g r u) -> p g r u", g=PASSES, u=2),
+                in_=flipped[:].rearrange("p g u r -> p g r u"),
+            )
             nc.vector.quantize_mx(
-                out=x_codes[:, j, :].bitcast(FP8X4), scales=x_scales[:, j, :], in_=grouped[:]
+                out=x_codes[:, j, :].bitcast(FP8X4), scales=x_scales[:, j, :], in_=x_grouped[:, j, :]
             )
 
-        for i, proj in enumerate(projections):
+        def spread_bias(i):
+            spread = psum.tile([P, FEATURES], BF16, tag="bank")
             for nb in range(BANKS_PER_ROW):
                 cols = slice(BANK * nb, BANK * (nb + 1))
-                spread = psum.tile([P, BANK], F32, tag="bank")
                 nc.tensor.matmul(
-                    out=spread[:], lhsT=ones[:], rhs=bias_rows[:, i, cols], start=True, stop=True
+                    out=spread[:, cols], lhsT=ones[:], rhs=bias_rows[:, i, cols], start=True, stop=True
                 )
-                nc.scalar.copy(out=bias_all[:, i, cols], in_=spread[:])
+            nc.vector.tensor_copy(out=bias_all[:, i, :], in_=spread[:])
 
-            y = keep.tile([P, HEADS, TOKEN_TILES, HEAD_DIM], F32, name="y_" + proj["name"])
-            out_runs = proj["out"].rearrange(
-                "b h (c r j) d -> r h c b (j d)", r=TOKEN_TILES // STORE_TILES, j=STORE_TILES
-            )
-            for j in range(TOKEN_TILES):
-                accs = [
-                    psum.tile([P, BANK], F32, tag="bank", name="acc%d" % nb)
-                    for nb in range(BANKS_PER_ROW)
-                ]
-                for g in range(PASSES):
-                    tokens = slice(P * g, P * (g + 1))
-                    for nb in range(BANKS_PER_ROW):
-                        cols = slice(BANK * nb, BANK * (nb + 1))
-                        nc.tensor.matmul_mx(
-                            out=accs[nb][:],
-                            lhsT=x_codes[:, j, tokens].bitcast(FP8X4),
-                            lhsT_scale=x_scales[:, j, tokens],
-                            rhs=w_codes[:, i, g, cols].bitcast(FP8X4),
-                            rhs_scale=w_scales[SCALE_ROWS * g : P, i, cols],
-                            start=(g == 0),
-                            stop=(g == PASSES - 1),
-                        )
+        def multiply_and_add_bias(i, j):
+            accs = [
+                psum.tile([P, BANK], F32, tag="bank", name="acc%d" % nb)
+                for nb in range(BANKS_PER_ROW)
+            ]
+            for g in range(PASSES):
+                tokens = slice(P * g, P * (g + 1))
                 for nb in range(BANKS_PER_ROW):
                     cols = slice(BANK * nb, BANK * (nb + 1))
-                    heads = slice(HEADS_PER_BANK * nb, HEADS_PER_BANK * (nb + 1))
-                    nc.vector.tensor_tensor(
-                        out=y[:, heads, j, :],
-                        in0=accs[nb][:].rearrange("p (h d) -> p h d", d=HEAD_DIM),
-                        in1=bias_all[:, i, cols].rearrange("p (h d) -> p h d", d=HEAD_DIM),
-                        op=ALU.add,
+                    nc.tensor.matmul_mx(
+                        out=accs[nb][:],
+                        lhsT=x_codes[:, j, tokens].bitcast(FP8X4),
+                        lhsT_scale=x_scales[:, j, tokens],
+                        rhs=w_codes[:, i, g, cols].bitcast(FP8X4),
+                        rhs_scale=w_scales[SCALE_ROWS * g : P, i, cols],
+                        start=(g == 0),
+                        stop=(g == PASSES - 1),
                     )
-                if proj["normalise"]:
-                    squares = small.tile([P, HEADS, HEAD_DIM], F32)
-                    sum_squares = small.tile([P, 1], F32)
-                    nc.scalar.activation(
-                        out=squares[:], in_=y[:, :, j, :], func=ACT.Square, accum_out=sum_squares[:]
+            for nb in range(BANKS_PER_ROW):
+                cols = slice(BANK * nb, BANK * (nb + 1))
+                heads = slice(HEADS_PER_BANK * nb, HEADS_PER_BANK * (nb + 1))
+                nc.vector.tensor_tensor(
+                    out=y_all[:, i, heads, j, :],
+                    in0=accs[nb][:].rearrange("p (h d) -> p h d", d=HEAD_DIM),
+                    in1=bias_all[:, i, cols].rearrange("p (h d) -> p h d", d=HEAD_DIM),
+                    op=ALU.add,
+                )
+
+        def normalise(i, j):
+            squares = small.tile([P, HEADS, HEAD_DIM], F32)
+            sum_squares = small.tile([P, 1], F32)
+            nc.scalar.activation(
+                out=squares[:], in_=y_all[:, i, :, j, :], func=ACT.Square, accum_out=sum_squares[:]
+            )
+            excess = small.tile([P, 1], F32)
+            nc.scalar.activation(
+                out=excess[:], in_=sum_squares[:], func=ACT.Relu, bias=-NORM_FLOOR_SQUARED
+            )
+            inverse_norm = small.tile([P, 1], F32)
+            nc.scalar.activation(
+                out=inverse_norm[:], in_=excess[:], func=ACT.Abs_reciprocal_sqrt, bias=NORM_FLOOR_SQUARED
+            )
+            nc.gpsimd.tensor_scalar(
+                out=y_all[:, i, :, j, :],
+                in0=y_all[:, i, :, j, :],
+                scalar1=inverse_norm[:, 0:1],
+                scalar2=0.0,
+                op0=ALU.mult,
+                op1=ALU.add,
+            )
+
+        def store_if_run_complete(i, j):
+            if (j + 1) % STORE_TILES == 0:
+                out_runs = projections[i]["out"].rearrange(
+                    "b h (c r j) d -> r h c b (j d)", r=TOKEN_TILES // STORE_TILES, j=STORE_TILES
+                )
+                done = slice(j + 1 - STORE_TILES, j + 1)
+                for h in range(HEADS):
+                    nc.sync.dma_start(
+                        out=out_runs[j // STORE_TILES, h],
+                        in_=y_all[:, i, h, done, :].rearrange("p j d -> p (j d)"),
                     )
-                    above_floor = small.tile([P, 1], F32)
-                    nc.scalar.activation(
-                        out=above_floor[:], in_=sum_squares[:], func=ACT.Relu, bias=-NORM_FLOOR_SQUARED
-                    )
-                    inverse_norm = small.tile([P, 1], F32)
-                    nc.scalar.activation(
-                        out=inverse_norm[:],
-                        in_=above_floor[:],
-                        func=ACT.Abs_reciprocal_sqrt,
-                        bias=NORM_FLOOR_SQUARED,
-                    )
-                    nc.vector.tensor_scalar(
-                        out=y[:, :, j, :],
-                        in0=y[:, :, j, :],
-                        scalar1=inverse_norm[:, 0:1],
-                        scalar2=None,
-                        op0=ALU.mult,
-                    )
-                if (j + 1) % STORE_TILES == 0:
-                    done = slice(j + 1 - STORE_TILES, j + 1)
-                    for h in range(HEADS):
-                        nc.sync.dma_start(
-                            out=out_runs[j // STORE_TILES, h],
-                            in_=y[:, h, done, :].rearrange("p j d -> p (j d)"),
-                        )
+
+        for j in range(half_tiles):
+            quantise_x(j)
+        token_tiles = [(i, j) for i in range(count) for j in range(TOKEN_TILES)]
+        for step in range(len(token_tiles) + NORM_LAG):
+            if step < len(token_tiles):
+                i, j = token_tiles[step]
+                if j == 0:
+                    spread_bias(i)
+                multiply_and_add_bias(i, j)
+                if not projections[i]["normalise"]:
+                    store_if_run_complete(i, j)
+                if step == half_tiles - 1:
+                    for later in range(half_tiles, TOKEN_TILES):
+                        quantise_x(later)
+            if step >= NORM_LAG:
+                i, j = token_tiles[step - NORM_LAG]
+                if projections[i]["normalise"]:
+                    normalise(i, j)
+                    store_if_run_complete(i, j)

@@ -29,7 +29,7 @@ WORDS_PER_PASS = K_PASS // 2
 SCALE_ROWS = 4
 QUADRANTS = 4
 STORE_TILES = 2
-NORM_LAG = 3
+NORM_LAG = 2
 NORM_FLOOR_SQUARED = 1e-24
 
 FLOPS = 2 * BATCH * SEQ * EMBED * 3 * FEATURES
@@ -87,14 +87,15 @@ def tile_knnxlmultiheadsattention_pa_kernel(
             out=table_warmer[:, 1:2], in_=table_warmer[:, 0:1], func=ACT.Abs_reciprocal_sqrt
         )
 
-        half_tiles = TOKEN_TILES // 2
-        x_by_half = x.rearrange("b (c half je) e -> half c b (je e)", half=2, je=half_tiles)
+        x_runs = x.rearrange(
+            "b (c r j) e -> r c b (j e)", r=TOKEN_TILES // STORE_TILES, j=STORE_TILES
+        )
+        for r in range(TOKEN_TILES // STORE_TILES):
+            nc.sync.dma_start(
+                out=x_sb[:, STORE_TILES * r : STORE_TILES * (r + 1), :].rearrange("p j e -> p (j e)"),
+                in_=x_runs[r],
+            )
         for i, proj in enumerate(projections):
-            if i < 2:
-                nc.sync.dma_start(
-                    out=x_sb[:, half_tiles * i : half_tiles * (i + 1), :].rearrange("p j e -> p (j e)"),
-                    in_=x_by_half[i],
-                )
             nc.sync.dma_start(
                 out=bias_rows[0:1, i, :], in_=proj["bias"].rearrange("(o n) -> o n", o=1)
             )
@@ -122,7 +123,7 @@ def tile_knnxlmultiheadsattention_pa_kernel(
                         x_words[:, j, WORDS_PER_PASS * g + u : WORDS_PER_PASS * (g + 1) : 2],
                         identity[:],
                     )
-            nc.vector.tensor_copy(
+            nc.scalar.copy(
                 out=x_grouped[:, j, :].bitcast(F32).rearrange("p (g r u) -> p g r u", g=PASSES, u=2),
                 in_=flipped[:].rearrange("p g u r -> p g r u"),
             )
@@ -202,9 +203,14 @@ def tile_knnxlmultiheadsattention_pa_kernel(
                         in_=y_all[:, i, h, done, :].rearrange("p j d -> p (j d)"),
                     )
 
-        for j in range(half_tiles):
+        for j in range(TOKEN_TILES):
             quantise_x(j)
-        token_tiles = [(i, j) for i in range(count) for j in range(TOKEN_TILES)]
+        token_tiles = [
+            (i, j)
+            for r in range(TOKEN_TILES // STORE_TILES)
+            for i in range(count)
+            for j in range(STORE_TILES * r, STORE_TILES * (r + 1))
+        ]
         for step in range(len(token_tiles) + NORM_LAG):
             if step < len(token_tiles):
                 i, j = token_tiles[step]
@@ -213,9 +219,6 @@ def tile_knnxlmultiheadsattention_pa_kernel(
                 multiply_and_add_bias(i, j)
                 if not projections[i]["normalise"]:
                     store_if_run_complete(i, j)
-                if step == half_tiles - 1:
-                    for later in range(half_tiles, TOKEN_TILES):
-                        quantise_x(later)
             if step >= NORM_LAG:
                 i, j = token_tiles[step - NORM_LAG]
                 if projections[i]["normalise"]:

@@ -193,14 +193,14 @@ def tile_knnxlmultiheadsattention_pa_kernel(
 
         def store_if_run_complete(i, j):
             if (j + 1) % STORE_TILES == 0:
-                out_runs = projections[i]["out"].rearrange(
-                    "b h (c r j) d -> r h c b (j d)", r=TOKEN_TILES // STORE_TILES, j=STORE_TILES
-                )
                 done = slice(j + 1 - STORE_TILES, j + 1)
-                for h in range(HEADS):
+                for b in range(BATCH):
+                    out_runs = projections[i]["out"][b].rearrange(
+                        "h (c r j) d -> r c h (j d)", r=TOKEN_TILES // STORE_TILES, j=STORE_TILES
+                    )
                     nc.sync.dma_start(
-                        out=out_runs[j // STORE_TILES, h],
-                        in_=y_all[:, i, h, done, :].rearrange("p j d -> p (j d)"),
+                        out=out_runs[j // STORE_TILES],
+                        in_=y_all[b:P:BATCH, i, :, done, :].rearrange("p h j d -> p h (j d)"),
                     )
 
         for j in range(TOKEN_TILES):

@@ -87,13 +87,10 @@ def tile_knnxlmultiheadsattention_pa_kernel(
             out=table_warmer[:, 1:2], in_=table_warmer[:, 0:1], func=ACT.Abs_reciprocal_sqrt
         )
 
-        x_runs = x.rearrange(
-            "b (c r j) e -> r c b (j e)", r=TOKEN_TILES // STORE_TILES, j=STORE_TILES
-        )
-        for r in range(TOKEN_TILES // STORE_TILES):
+        for b in range(BATCH):
             nc.sync.dma_start(
-                out=x_sb[:, STORE_TILES * r : STORE_TILES * (r + 1), :].rearrange("p j e -> p (j e)"),
-                in_=x_runs[r],
+                out=x_sb[:, STORE_TILES * b : STORE_TILES * (b + 1), :].rearrange("p j e -> p (j e)"),
+                in_=x[b].rearrange("(c j) e -> c (j e)", j=STORE_TILES),
             )
         for i, proj in enumerate(projections):
             nc.sync.dma_start(
@@ -194,14 +191,12 @@ def tile_knnxlmultiheadsattention_pa_kernel(
         def store_if_run_complete(i, j):
             if (j + 1) % STORE_TILES == 0:
                 done = slice(j + 1 - STORE_TILES, j + 1)
-                for b in range(BATCH):
-                    out_runs = projections[i]["out"][b].rearrange(
-                        "h (c r j) d -> r c h (j d)", r=TOKEN_TILES // STORE_TILES, j=STORE_TILES
-                    )
-                    nc.sync.dma_start(
-                        out=out_runs[j // STORE_TILES],
-                        in_=y_all[b:P:BATCH, i, :, done, :].rearrange("p h j d -> p h (j d)"),
-                    )
+                nc.sync.dma_start(
+                    out=projections[i]["out"][j // STORE_TILES].rearrange(
+                        "h (c j) d -> c h (j d)", j=STORE_TILES
+                    ),
+                    in_=y_all[:, i, :, done, :].rearrange("p h j d -> p h (j d)"),
+                )
 
         for j in range(TOKEN_TILES):
             quantise_x(j)

@@ -32,6 +32,8 @@ STORE_TILES = 2
 NORM_LAG = 2
 NORM_FLOOR_SQUARED = 1e-24
 
+IDLE_MATMULS = 6
+
 FLOPS = 2 * BATCH * SEQ * EMBED * 3 * FEATURES
 
 
@@ -77,25 +79,38 @@ def tile_knnxlmultiheadsattention_pa_kernel(
         ones = keep.tile([P, P], BF16)
         identity = keep.tile([P, P], F32)
         table_warmer = keep.tile([P, 2], F32)
+        idle_rhs = keep.tile([P, BANK], BF16)
 
-        nc.vector.memset(bias_rows[:].bitcast(I32), 0)
-        nc.vector.memset(w_scales[:].bitcast(I32), 0)
-        nc.vector.memset(table_warmer[:], 1.0)
+        nc.vector.memset(bias_rows[:, 0, :].bitcast(I32), 0)
         nc.vector.memset(ones[:], 1.0)
+        nc.vector.memset(idle_rhs[:], 0.0)
+        nc.vector.memset(w_scales[:, 0, :].bitcast(I32), 0)
+        nc.vector.memset(table_warmer[:], 1.0)
+        nc.vector.memset(bias_rows[:, 1:, :].rearrange("p i n -> p (i n)").bitcast(I32), 0)
+        nc.vector.memset(w_scales[:, 1:, :].rearrange("p i n -> p (i n)").bitcast(I32), 0)
         make_identity(nc, identity[:])
+        idle_bank = psum.tile([P, BANK], F32, tag="bank")
+        for n in range(IDLE_MATMULS):
+            nc.tensor.matmul(out=idle_bank[:], lhsT=ones[:], rhs=idle_rhs[:], start=True, stop=True)
         nc.scalar.activation(
             out=table_warmer[:, 1:2], in_=table_warmer[:, 0:1], func=ACT.Abs_reciprocal_sqrt
         )
+
+        def load_bias(i):
+            nc.sync.dma_start(
+                out=bias_rows[0:1, i, :], in_=projections[i]["bias"].rearrange("(o n) -> o n", o=1)
+            )
 
         for b in range(BATCH):
             nc.sync.dma_start(
                 out=x_sb[:, STORE_TILES * b : STORE_TILES * (b + 1), :].rearrange("p j e -> p (j e)"),
                 in_=x[b].rearrange("(c j) e -> c (j e)", j=STORE_TILES),
             )
+            if b == 0:
+                load_bias(0)
         for i, proj in enumerate(projections):
-            nc.sync.dma_start(
-                out=bias_rows[0:1, i, :], in_=proj["bias"].rearrange("(o n) -> o n", o=1)
-            )
+            if i > 0:
+                load_bias(i)
             for quadrant in range(QUADRANTS):
                 first = 32 * quadrant
                 rows = slice(SCALE_ROWS * quadrant, SCALE_ROWS * (quadrant + 1))
@@ -165,57 +180,90 @@ def tile_knnxlmultiheadsattention_pa_kernel(
                     op=ALU.add,
                 )
 
-        def normalise(i, j):
+        def square_sum(i, j, sums):
             squares = small.tile([P, HEADS, HEAD_DIM], F32)
-            sum_squares = small.tile([P, 1], F32)
+            column = j % STORE_TILES
             nc.scalar.activation(
-                out=squares[:], in_=y_all[:, i, :, j, :], func=ACT.Square, accum_out=sum_squares[:]
+                out=squares[:],
+                in_=y_all[:, i, :, j, :],
+                func=ACT.Square,
+                accum_out=sums[:, column : column + 1],
             )
+
+        def invert_norm(j, sums, inverse):
+            column = slice(j % STORE_TILES, j % STORE_TILES + 1)
             excess = small.tile([P, 1], F32)
             nc.scalar.activation(
-                out=excess[:], in_=sum_squares[:], func=ACT.Relu, bias=-NORM_FLOOR_SQUARED
+                out=excess[:], in_=sums[:, column], func=ACT.Relu, bias=-NORM_FLOOR_SQUARED
             )
-            inverse_norm = small.tile([P, 1], F32)
             nc.scalar.activation(
-                out=inverse_norm[:], in_=excess[:], func=ACT.Abs_reciprocal_sqrt, bias=NORM_FLOOR_SQUARED
+                out=inverse[:, column], in_=excess[:], func=ACT.Abs_reciprocal_sqrt, bias=NORM_FLOOR_SQUARED
             )
+
+        def scale_on_gpsimd(i, j, inverse):
+            column = j % STORE_TILES
             nc.gpsimd.tensor_scalar(
                 out=y_all[:, i, :, j, :],
                 in0=y_all[:, i, :, j, :],
-                scalar1=inverse_norm[:, 0:1],
+                scalar1=inverse[:, column : column + 1],
                 scalar2=0.0,
                 op0=ALU.mult,
                 op1=ALU.add,
             )
 
-        def store_if_run_complete(i, j):
-            if (j + 1) % STORE_TILES == 0:
-                done = slice(j + 1 - STORE_TILES, j + 1)
-                nc.sync.dma_start(
-                    out=projections[i]["out"][j // STORE_TILES].rearrange(
-                        "h (c j) d -> c h (j d)", j=STORE_TILES
-                    ),
-                    in_=y_all[:, i, :, done, :].rearrange("p h j d -> p h (j d)"),
-                )
+        def scale_on_vector(i, j, inverse):
+            column = j % STORE_TILES
+            nc.vector.tensor_scalar(
+                out=y_all[:, i, :, j, :],
+                in0=y_all[:, i, :, j, :],
+                scalar1=inverse[:, column : column + 1],
+                scalar2=None,
+                op0=ALU.mult,
+            )
+
+        def store(i, b):
+            nc.sync.dma_start(
+                out=projections[i]["out"][b].rearrange("h (c j) d -> c h (j d)", j=STORE_TILES),
+                in_=y_all[:, i, :, STORE_TILES * b : STORE_TILES * (b + 1), :].rearrange(
+                    "p h j d -> p h (j d)"
+                ),
+            )
 
         for j in range(TOKEN_TILES):
             quantise_x(j)
-        token_tiles = [
-            (i, j)
-            for r in range(TOKEN_TILES // STORE_TILES)
-            for i in range(count)
-            for j in range(STORE_TILES * r, STORE_TILES * (r + 1))
-        ]
-        for step in range(len(token_tiles) + NORM_LAG):
-            if step < len(token_tiles):
-                i, j = token_tiles[step]
-                if j == 0:
+            if j == STORE_TILES - 1:
+                spread_bias(0)
+        pairs = [(0, 0), (1, 0), (2, 0), (0, 1), (1, 1), (2, 1)]
+        spread = [0]
+        waiting = []
+        for step in range(len(pairs) + 1):
+            if step < len(pairs):
+                i, b = pairs[step]
+                tiles = list(range(STORE_TILES * b, STORE_TILES * (b + 1)))
+                if i not in spread:
+                    spread.append(i)
                     spread_bias(i)
-                multiply_and_add_bias(i, j)
-                if not projections[i]["normalise"]:
-                    store_if_run_complete(i, j)
-            if step >= NORM_LAG:
-                i, j = token_tiles[step - NORM_LAG]
                 if projections[i]["normalise"]:
-                    normalise(i, j)
-                    store_if_run_complete(i, j)
+                    last_norm = all(not projections[n]["normalise"] for n, m in pairs[step + 1 :])
+                    on_vector = tiles[2:] if last_norm else []
+                    sums = small.tile([P, STORE_TILES], F32)
+                    inverse = small.tile([P, STORE_TILES], F32)
+                    for j in tiles:
+                        multiply_and_add_bias(i, j)
+                        square_sum(i, j, sums)
+                        invert_norm(j, sums, inverse)
+                        if j not in on_vector:
+                            scale_on_gpsimd(i, j, inverse)
+                    new_waiting = [(i, b, inverse, on_vector)]
+                else:
+                    for j in tiles:
+                        multiply_and_add_bias(i, j)
+                    store(i, b)
+                    new_waiting = []
+            else:
+                new_waiting = []
+            for i, b, inverse, on_vector in waiting:
+                for j in on_vector:
+                    scale_on_vector(i, j, inverse)
+                store(i, b)
+            waiting = new_waiting

@@ -32,7 +32,7 @@ STORE_TILES = 2
 NORM_LAG = 2
 NORM_FLOOR_SQUARED = 1e-24
 
-IDLE_MATMULS = 6
+IDLE_MATMULS = 4
 
 FLOPS = 2 * BATCH * SEQ * EMBED * 3 * FEATURES
 

@@ -60,6 +60,9 @@ def tile_knnxlmultiheadsattention_pa_kernel(
         dict(name="v", words=wv_words, scales=wv_scales, bias=bv, out=out_v, normalise=False),
     ]
     count = len(projections)
+    head_groups = [
+        slice(HEADS_PER_BANK * nb, HEADS_PER_BANK * (nb + 1)) for nb in range(BANKS_PER_ROW)
+    ]
 
     with ExitStack() as stack:
         keep = stack.enter_context(tc.tile_pool(name="keep", bufs=1))
@@ -200,34 +203,37 @@ def tile_knnxlmultiheadsattention_pa_kernel(
                 out=inverse[:, column], in_=excess[:], func=ACT.Abs_reciprocal_sqrt, bias=NORM_FLOOR_SQUARED
             )
 
-        def scale_on_gpsimd(i, j, inverse):
+        def scale_on_gpsimd(i, j, inverse, heads):
             column = j % STORE_TILES
             nc.gpsimd.tensor_scalar(
-                out=y_all[:, i, :, j, :],
-                in0=y_all[:, i, :, j, :],
+                out=y_all[:, i, heads, j, :],
+                in0=y_all[:, i, heads, j, :],
                 scalar1=inverse[:, column : column + 1],
                 scalar2=0.0,
                 op0=ALU.mult,
                 op1=ALU.add,
             )
 
-        def scale_on_vector(i, j, inverse):
+        def scale_on_vector(i, j, inverse, heads):
             column = j % STORE_TILES
             nc.vector.tensor_scalar(
-                out=y_all[:, i, :, j, :],
-                in0=y_all[:, i, :, j, :],
+                out=y_all[:, i, heads, j, :],
+                in0=y_all[:, i, heads, j, :],
                 scalar1=inverse[:, column : column + 1],
                 scalar2=None,
                 op0=ALU.mult,
             )
 
         def store(i, b):
-            nc.sync.dma_start(
-                out=projections[i]["out"][b].rearrange("h (c j) d -> c h (j d)", j=STORE_TILES),
-                in_=y_all[:, i, :, STORE_TILES * b : STORE_TILES * (b + 1), :].rearrange(
-                    "p h j d -> p h (j d)"
-                ),
-            )
+            for heads in head_groups:
+                nc.sync.dma_start(
+                    out=projections[i]["out"][b][heads].rearrange(
+                        "h (c j) d -> c h (j d)", j=STORE_TILES
+                    ),
+                    in_=y_all[:, i, heads, STORE_TILES * b : STORE_TILES * (b + 1), :].rearrange(
+                        "p h j d -> p h (j d)"
+                    ),
+                )
 
         for j in range(TOKEN_TILES):
             quantise_x(j)
@@ -245,7 +251,7 @@ def tile_knnxlmultiheadsattention_pa_kernel(
                     spread_bias(i)
                 if projections[i]["normalise"]:
                     last_norm = all(not projections[n]["normalise"] for n, m in pairs[step + 1 :])
-                    on_vector = tiles[2:] if last_norm else []
+                    on_vector = tiles[1:] if last_norm else []
                     sums = small.tile([P, STORE_TILES], F32)
                     inverse = small.tile([P, STORE_TILES], F32)
                     for j in tiles:
@@ -253,7 +259,8 @@ def tile_knnxlmultiheadsattention_pa_kernel(
                         square_sum(i, j, sums)
                         invert_norm(j, sums, inverse)
                         if j not in on_vector:
-                            scale_on_gpsimd(i, j, inverse)
+                            for heads in head_groups if j == tiles[-1] else [slice(0, HEADS)]:
+                                scale_on_gpsimd(i, j, inverse, heads)
                     new_waiting = [(i, b, inverse, on_vector)]
                 else:
                     for j in tiles:
@@ -264,6 +271,7 @@ def tile_knnxlmultiheadsattention_pa_kernel(
                 new_waiting = []
             for i, b, inverse, on_vector in waiting:
                 for j in on_vector:
-                    scale_on_vector(i, j, inverse)
+                    for heads in head_groups:
+                        scale_on_vector(i, j, inverse, heads)
                 store(i, b)
             waiting = new_waiting

@@ -251,7 +251,7 @@ def tile_knnxlmultiheadsattention_pa_kernel(
                     spread_bias(i)
                 if projections[i]["normalise"]:
                     last_norm = all(not projections[n]["normalise"] for n, m in pairs[step + 1 :])
-                    on_vector = tiles[1:] if last_norm else []
+                    on_vector = tiles[2:] if last_norm else []
                     sums = small.tile([P, STORE_TILES], F32)
                     inverse = small.tile([P, STORE_TILES], F32)
                     for j in tiles:

@@ -27,7 +27,6 @@ BANKS_PER_ROW = FEATURES // BANK
 HEADS_PER_BANK = BANK // HEAD_DIM
 WORDS_PER_PASS = K_PASS // 2
 SCALE_ROWS = 4
-QUADRANTS = 4
 STORE_TILES = 2
 NORM_LAG = 2
 NORM_FLOOR_SQUARED = 1e-24
@@ -75,7 +74,7 @@ def tile_knnxlmultiheadsattention_pa_kernel(
         x_codes = keep.tile([P, TOKEN_TILES, PASSES * P], U32, align_bytes=64)
         x_scales = keep.tile([P, TOKEN_TILES, PASSES * P], U8, align_bytes=64)
         w_codes = keep.tile([P, count, PASSES, FEATURES], I32, align_bytes=64)
-        w_scales = keep.tile([P, count, FEATURES], U8, align_bytes=64)
+        w_scales = keep.tile([P, count, PASSES, FEATURES], U8, align_bytes=64)
         bias_rows = keep.tile([P, count, FEATURES], BF16)
         bias_all = keep.tile([P, count, FEATURES], BF16)
         y_all = keep.tile([P, count, HEADS, TOKEN_TILES, HEAD_DIM], F32)
@@ -87,10 +86,10 @@ def tile_knnxlmultiheadsattention_pa_kernel(
         nc.vector.memset(bias_rows[:, 0, :].bitcast(I32), 0)
         nc.vector.memset(ones[:], 1.0)
         nc.vector.memset(idle_rhs[:], 0.0)
-        nc.vector.memset(w_scales[:, 0, :].bitcast(I32), 0)
+        nc.vector.memset(w_scales[:, 0, :, :].rearrange("p g n -> p (g n)").bitcast(I32), 0)
         nc.vector.memset(table_warmer[:], 1.0)
         nc.vector.memset(bias_rows[:, 1:, :].rearrange("p i n -> p (i n)").bitcast(I32), 0)
-        nc.vector.memset(w_scales[:, 1:, :].rearrange("p i n -> p (i n)").bitcast(I32), 0)
+        nc.vector.memset(w_scales[:, 1:, :, :].rearrange("p i g n -> p (i g n)").bitcast(I32), 0)
         make_identity(nc, identity[:])
         idle_bank = psum.tile([P, BANK], F32, tag="bank")
         for n in range(IDLE_MATMULS):
@@ -114,12 +113,11 @@ def tile_knnxlmultiheadsattention_pa_kernel(
         for i, proj in enumerate(projections):
             if i > 0:
                 load_bias(i)
-            for quadrant in range(QUADRANTS):
-                first = 32 * quadrant
-                rows = slice(SCALE_ROWS * quadrant, SCALE_ROWS * (quadrant + 1))
+            by_row = proj["scales"].rearrange("g (q r) n -> r q g n", r=SCALE_ROWS)
+            for r in range(SCALE_ROWS):
                 nc.sync.dma_start(
-                    out=w_scales[first : first + PASSES * SCALE_ROWS, i, :].bitcast(I32),
-                    in_=proj["scales"][:, rows, :].bitcast(I32),
+                    out=w_scales[SCALE_ROWS * i + r : P : 32, i, :, :].bitcast(I32),
+                    in_=by_row[r].bitcast(I32),
                 )
             for g in range(PASSES):
                 nc.sync.dma_start(
@@ -169,7 +167,7 @@ def tile_knnxlmultiheadsattention_pa_kernel(
                         lhsT=x_codes[:, j, tokens].bitcast(FP8X4),
                         lhsT_scale=x_scales[:, j, tokens],
                         rhs=w_codes[:, i, g, cols].bitcast(FP8X4),
-                        rhs_scale=w_scales[SCALE_ROWS * g : P, i, cols],
+                        rhs_scale=w_scales[SCALE_ROWS * i : P, i, g, cols],
                         start=(g == 0),
                         stop=(g == PASSES - 1),
                     )

@@ -27,8 +27,8 @@ BANKS_PER_ROW = FEATURES // BANK
 HEADS_PER_BANK = BANK // HEAD_DIM
 WORDS_PER_PASS = K_PASS // 2
 SCALE_ROWS = 4
-STORE_TILES = 2
-NORM_LAG = 2
+QUADRANTS = 4
+PAIR = 2
 NORM_FLOOR_SQUARED = 1e-24
 
 IDLE_MATMULS = 4
@@ -54,10 +54,11 @@ def tile_knnxlmultiheadsattention_pa_kernel(
 ):
     nc = tc.nc
     projections = [
-        dict(name="q", words=wq_words, scales=wq_scales, bias=bq, out=out_q, normalise=True),
-        dict(name="k", words=wk_words, scales=wk_scales, bias=bk, out=out_k, normalise=True),
-        dict(name="v", words=wv_words, scales=wv_scales, bias=bv, out=out_v, normalise=False),
+        dict(words=wv_words, scales=wv_scales, bias=bv, out=out_v),
+        dict(words=wq_words, scales=wq_scales, bias=bq, out=out_q),
+        dict(words=wk_words, scales=wk_scales, bias=bk, out=out_k),
     ]
+    V, Q, K = range(len(projections))
     count = len(projections)
     head_groups = [
         slice(HEADS_PER_BANK * nb, HEADS_PER_BANK * (nb + 1)) for nb in range(BANKS_PER_ROW)
@@ -103,31 +104,33 @@ def tile_knnxlmultiheadsattention_pa_kernel(
                 out=bias_rows[0:1, i, :], in_=projections[i]["bias"].rearrange("(o n) -> o n", o=1)
             )
 
-        for b in range(BATCH):
+        for pair in range(TOKEN_TILES // PAIR):
+            tiles = slice(PAIR * pair, PAIR * (pair + 1))
             nc.sync.dma_start(
-                out=x_sb[:, STORE_TILES * b : STORE_TILES * (b + 1), :].rearrange("p j e -> p (j e)"),
-                in_=x[b].rearrange("(c j) e -> c (j e)", j=STORE_TILES),
+                out=x_sb[:, tiles, :].rearrange("p j e -> p (j e)"),
+                in_=x.rearrange("b (c h j) e -> h c b (j e)", h=TOKEN_TILES // PAIR, j=PAIR)[pair],
             )
-            if b == 0:
-                load_bias(0)
         for i, proj in enumerate(projections):
-            if i > 0:
-                load_bias(i)
-            by_row = proj["scales"].rearrange("g (q r) n -> r q g n", r=SCALE_ROWS)
-            for r in range(SCALE_ROWS):
+            load_bias(i)
+            by_quadrant = proj["scales"].rearrange("g (q r) n -> q r g n", r=SCALE_ROWS)
+            for quadrant in range(QUADRANTS):
+                first = 32 * quadrant + SCALE_ROWS * i
                 nc.sync.dma_start(
-                    out=w_scales[SCALE_ROWS * i + r : P : 32, i, :, :].bitcast(I32),
-                    in_=by_row[r].bitcast(I32),
+                    out=w_scales[first : first + SCALE_ROWS, i, :, :].bitcast(I32),
+                    in_=by_quadrant[quadrant].bitcast(I32),
                 )
-            for g in range(PASSES):
-                nc.sync.dma_start(
-                    out=w_codes[:, i, g, :],
-                    in_=proj["words"][g].rearrange("p n t -> p (n t)").bitcast(I32),
-                )
+            words = proj["words"].rearrange("g p n t -> p g (n t)").bitcast(I32)
+            if i == V:
+                for nb in range(BANKS_PER_ROW):
+                    cols = slice(BANK * nb, BANK * (nb + 1))
+                    nc.sync.dma_start(out=w_codes[:, i, :, cols], in_=words[:, :, cols])
+            else:
+                for g in range(PASSES):
+                    nc.sync.dma_start(out=w_codes[:, i, g, :], in_=words[:, g, :])
 
         x_words = x_sb[:].bitcast(F32)
 
-        def quantise_x(j):
+        def turn_x(j):
             flipped = psum.tile([P, PASSES, 2, P], F32, tag="bank")
             for g in range(PASSES):
                 for u in range(2):
@@ -140,30 +143,29 @@ def tile_knnxlmultiheadsattention_pa_kernel(
                 out=x_grouped[:, j, :].bitcast(F32).rearrange("p (g r u) -> p g r u", g=PASSES, u=2),
                 in_=flipped[:].rearrange("p g u r -> p g r u"),
             )
+
+        def quantise_x(j):
             nc.vector.quantize_mx(
                 out=x_codes[:, j, :].bitcast(FP8X4), scales=x_scales[:, j, :], in_=x_grouped[:, j, :]
             )
 
-        def spread_bias(i):
+        def spread_bias(i, copy):
             spread = psum.tile([P, FEATURES], BF16, tag="bank")
             for nb in range(BANKS_PER_ROW):
                 cols = slice(BANK * nb, BANK * (nb + 1))
                 nc.tensor.matmul(
                     out=spread[:, cols], lhsT=ones[:], rhs=bias_rows[:, i, cols], start=True, stop=True
                 )
-            nc.vector.tensor_copy(out=bias_all[:, i, :], in_=spread[:])
+            copy(out=bias_all[:, i, :], in_=spread[:])
 
-        def multiply_and_add_bias(i, j):
-            accs = [
-                psum.tile([P, BANK], F32, tag="bank", name="acc%d" % nb)
-                for nb in range(BANKS_PER_ROW)
-            ]
+        def multiply(i, j, banks):
+            accs = [psum.tile([P, BANK], F32, tag="bank", name="acc%d" % nb) for nb in banks]
             for g in range(PASSES):
                 tokens = slice(P * g, P * (g + 1))
-                for nb in range(BANKS_PER_ROW):
+                for acc, nb in zip(accs, banks):
                     cols = slice(BANK * nb, BANK * (nb + 1))
                     nc.tensor.matmul_mx(
-                        out=accs[nb][:],
+                        out=acc[:],
                         lhsT=x_codes[:, j, tokens].bitcast(FP8X4),
                         lhsT_scale=x_scales[:, j, tokens],
                         rhs=w_codes[:, i, g, cols].bitcast(FP8X4),
@@ -171,105 +173,113 @@ def tile_knnxlmultiheadsattention_pa_kernel(
                         start=(g == 0),
                         stop=(g == PASSES - 1),
                     )
-            for nb in range(BANKS_PER_ROW):
+            return accs
+
+        def multiply_and_add_bias(i, j, banks):
+            for acc, nb in zip(multiply(i, j, banks), banks):
                 cols = slice(BANK * nb, BANK * (nb + 1))
-                heads = slice(HEADS_PER_BANK * nb, HEADS_PER_BANK * (nb + 1))
                 nc.vector.tensor_tensor(
-                    out=y_all[:, i, heads, j, :],
-                    in0=accs[nb][:].rearrange("p (h d) -> p h d", d=HEAD_DIM),
+                    out=y_all[:, i, head_groups[nb], j, :],
+                    in0=acc[:].rearrange("p (h d) -> p h d", d=HEAD_DIM),
                     in1=bias_all[:, i, cols].rearrange("p (h d) -> p h d", d=HEAD_DIM),
                     op=ALU.add,
                 )
 
-        def square_sum(i, j, sums):
+        def multiply_then_add_bias(i, j, nb):
+            cols = slice(BANK * nb, BANK * (nb + 1))
+            acc = multiply(i, j, [nb])[0]
+            y = y_all[:, i, head_groups[nb], j, :]
+            nc.scalar.copy(out=y, in_=acc[:].rearrange("p (h d) -> p h d", d=HEAD_DIM))
+            nc.gpsimd.tensor_tensor(
+                out=y, in0=y, in1=bias_all[:, i, cols].rearrange("p (h d) -> p h d", d=HEAD_DIM), op=ALU.add
+            )
+
+        def square_sum(i, j, heads, total):
             squares = small.tile([P, HEADS, HEAD_DIM], F32)
-            column = j % STORE_TILES
             nc.scalar.activation(
-                out=squares[:],
-                in_=y_all[:, i, :, j, :],
-                func=ACT.Square,
-                accum_out=sums[:, column : column + 1],
+                out=squares[:, heads, :], in_=y_all[:, i, heads, j, :], func=ACT.Square, accum_out=total
             )
 
-        def invert_norm(j, sums, inverse):
-            column = slice(j % STORE_TILES, j % STORE_TILES + 1)
-            excess = small.tile([P, 1], F32)
+        def invert_norms(excess):
+            inverse = small.tile([P, PAIR], F32)
             nc.scalar.activation(
-                out=excess[:], in_=sums[:, column], func=ACT.Relu, bias=-NORM_FLOOR_SQUARED
+                out=inverse[:], in_=excess[:], func=ACT.Abs_reciprocal_sqrt, bias=NORM_FLOOR_SQUARED
             )
-            nc.scalar.activation(
-                out=inverse[:, column], in_=excess[:], func=ACT.Abs_reciprocal_sqrt, bias=NORM_FLOOR_SQUARED
-            )
+            return inverse
 
-        def scale_on_gpsimd(i, j, inverse, heads):
-            column = j % STORE_TILES
-            nc.gpsimd.tensor_scalar(
-                out=y_all[:, i, heads, j, :],
-                in0=y_all[:, i, heads, j, :],
-                scalar1=inverse[:, column : column + 1],
-                scalar2=0.0,
-                op0=ALU.mult,
-                op1=ALU.add,
-            )
-
-        def scale_on_vector(i, j, inverse, heads):
-            column = j % STORE_TILES
-            nc.vector.tensor_scalar(
-                out=y_all[:, i, heads, j, :],
-                in0=y_all[:, i, heads, j, :],
-                scalar1=inverse[:, column : column + 1],
-                scalar2=None,
-                op0=ALU.mult,
-            )
-
-        def store(i, b):
+        def scale(i, pair, inverse):
             for heads in head_groups:
-                nc.sync.dma_start(
-                    out=projections[i]["out"][b][heads].rearrange(
-                        "h (c j) d -> c h (j d)", j=STORE_TILES
-                    ),
-                    in_=y_all[:, i, heads, STORE_TILES * b : STORE_TILES * (b + 1), :].rearrange(
-                        "p h j d -> p h (j d)"
-                    ),
+                for n in range(PAIR):
+                    y = y_all[:, i, heads, PAIR * pair + n, :]
+                    nc.gpsimd.tensor_scalar(
+                        out=y,
+                        in0=y,
+                        scalar1=inverse[:, n : n + 1],
+                        scalar2=0.0,
+                        op0=ALU.mult,
+                        op1=ALU.add,
+                    )
+
+        def first_normalised_pair(i):
+            halves = [small.tile([P, PAIR], F32, name="half%d" % nb) for nb in range(BANKS_PER_ROW)]
+            lowered = small.tile([P, PAIR], F32)
+            excess = small.tile([P, PAIR], F32)
+            for nb in range(BANKS_PER_ROW):
+                for n in range(PAIR):
+                    multiply_and_add_bias(i, n, [nb])
+                    square_sum(i, n, head_groups[nb], halves[nb][:, n : n + 1])
+                if nb == 0:
+                    nc.scalar.activation(
+                        out=lowered[:], in_=halves[0][:], func=ACT.Identity, bias=-NORM_FLOOR_SQUARED
+                    )
+            for n in range(PAIR):
+                nc.scalar.activation(
+                    out=excess[:, n : n + 1],
+                    in_=halves[1][:, n : n + 1],
+                    func=ACT.Relu,
+                    bias=lowered[:, n : n + 1],
                 )
+            scale(i, 0, invert_norms(excess))
+
+        def normalised_pair(i, pair):
+            sums = small.tile([P, PAIR], F32)
+            excess = small.tile([P, PAIR], F32)
+            for n in range(PAIR):
+                multiply_and_add_bias(i, PAIR * pair + n, range(BANKS_PER_ROW))
+                square_sum(i, PAIR * pair + n, slice(0, HEADS), sums[:, n : n + 1])
+            nc.scalar.activation(
+                out=excess[:], in_=sums[:], func=ACT.Relu, bias=-NORM_FLOOR_SQUARED
+            )
+            scale(i, pair, invert_norms(excess))
+
+        def store(i, tiles):
+            for heads in head_groups:
+                for b in range(BATCH):
+                    out = projections[i]["out"][b][heads].rearrange(
+                        "h (c j) d -> c h j d", j=TOKEN_TILES
+                    )
+                    nc.sync.dma_start(
+                        out=out[:, :, tiles, :].rearrange("c h j d -> c h (j d)"),
+                        in_=y_all[b:P:BATCH, i, heads, tiles, :].rearrange("p h j d -> p h (j d)"),
+                    )
 
         for j in range(TOKEN_TILES):
+            turn_x(j)
             quantise_x(j)
-            if j == STORE_TILES - 1:
-                spread_bias(0)
-        pairs = [(0, 0), (1, 0), (2, 0), (0, 1), (1, 1), (2, 1)]
-        spread = [0]
-        waiting = []
-        for step in range(len(pairs) + 1):
-            if step < len(pairs):
-                i, b = pairs[step]
-                tiles = list(range(STORE_TILES * b, STORE_TILES * (b + 1)))
-                if i not in spread:
-                    spread.append(i)
-                    spread_bias(i)
-                if projections[i]["normalise"]:
-                    last_norm = all(not projections[n]["normalise"] for n, m in pairs[step + 1 :])
-                    on_vector = tiles[2:] if last_norm else []
-                    sums = small.tile([P, STORE_TILES], F32)
-                    inverse = small.tile([P, STORE_TILES], F32)
-                    for j in tiles:
-                        multiply_and_add_bias(i, j)
-                        square_sum(i, j, sums)
-                        invert_norm(j, sums, inverse)
-                        if j not in on_vector:
-                            for heads in head_groups if j == tiles[-1] else [slice(0, HEADS)]:
-                                scale_on_gpsimd(i, j, inverse, heads)
-                    new_waiting = [(i, b, inverse, on_vector)]
-                else:
-                    for j in tiles:
-                        multiply_and_add_bias(i, j)
-                    store(i, b)
-                    new_waiting = []
-            else:
-                new_waiting = []
-            for i, b, inverse, on_vector in waiting:
-                for j in on_vector:
-                    for heads in head_groups:
-                        scale_on_vector(i, j, inverse, heads)
-                store(i, b)
-            waiting = new_waiting
+            if j == PAIR - 1:
+                spread_bias(V, nc.scalar.copy)
+        for nb in range(BANKS_PER_ROW):
+            for j in range(TOKEN_TILES - 1):
+                multiply_and_add_bias(V, j, [nb])
+                if nb == 0 and j == PAIR - 1:
+                    spread_bias(Q, nc.scalar.copy)
+            multiply_then_add_bias(V, TOKEN_TILES - 1, nb)
+        first_normalised_pair(Q)
+        normalised_pair(Q, 1)
+        spread_bias(K, nc.vector.tensor_copy)
+        normalised_pair(K, 0)
+        normalised_pair(K, 1)
+        store(V, slice(0, TOKEN_TILES))
+        for i in (Q, K):
+            for pair in range(TOKEN_TILES // PAIR):
+                store(i, slice(PAIR * pair, PAIR * (pair + 1)))

@@ -54,11 +54,11 @@ def tile_knnxlmultiheadsattention_pa_kernel(
 ):
     nc = tc.nc
     projections = [
-        dict(words=wv_words, scales=wv_scales, bias=bv, out=out_v),
         dict(words=wq_words, scales=wq_scales, bias=bq, out=out_q),
+        dict(words=wv_words, scales=wv_scales, bias=bv, out=out_v),
         dict(words=wk_words, scales=wk_scales, bias=bk, out=out_k),
     ]
-    V, Q, K = range(len(projections))
+    Q, V, K = range(len(projections))
     count = len(projections)
     head_groups = [
         slice(HEADS_PER_BANK * nb, HEADS_PER_BANK * (nb + 1)) for nb in range(BANKS_PER_ROW)
@@ -84,13 +84,13 @@ def tile_knnxlmultiheadsattention_pa_kernel(
         table_warmer = keep.tile([P, 2], F32)
         idle_rhs = keep.tile([P, BANK], BF16)
 
-        nc.vector.memset(bias_rows[:, 0, :].bitcast(I32), 0)
-        nc.vector.memset(ones[:], 1.0)
-        nc.vector.memset(idle_rhs[:], 0.0)
-        nc.vector.memset(w_scales[:, 0, :, :].rearrange("p g n -> p (g n)").bitcast(I32), 0)
-        nc.vector.memset(table_warmer[:], 1.0)
-        nc.vector.memset(bias_rows[:, 1:, :].rearrange("p i n -> p (i n)").bitcast(I32), 0)
-        nc.vector.memset(w_scales[:, 1:, :, :].rearrange("p i g n -> p (i g n)").bitcast(I32), 0)
+        for i in range(count):
+            nc.vector.memset(bias_rows[:, i, :].bitcast(I32), 0)
+            nc.vector.memset(w_scales[:, i, :, :].rearrange("p g n -> p (g n)").bitcast(I32), 0)
+            if i == Q:
+                nc.vector.memset(ones[:], 1.0)
+                nc.vector.memset(idle_rhs[:], 0.0)
+                nc.vector.memset(table_warmer[:], 1.0)
         make_identity(nc, identity[:])
         idle_bank = psum.tile([P, BANK], F32, tag="bank")
         for n in range(IDLE_MATMULS):
@@ -104,13 +104,17 @@ def tile_knnxlmultiheadsattention_pa_kernel(
                 out=bias_rows[0:1, i, :], in_=projections[i]["bias"].rearrange("(o n) -> o n", o=1)
             )
 
-        for pair in range(TOKEN_TILES // PAIR):
+        def load_x(pair):
             tiles = slice(PAIR * pair, PAIR * (pair + 1))
             nc.sync.dma_start(
                 out=x_sb[:, tiles, :].rearrange("p j e -> p (j e)"),
                 in_=x.rearrange("b (c h j) e -> h c b (j e)", h=TOKEN_TILES // PAIR, j=PAIR)[pair],
             )
+
+        load_x(0)
         for i, proj in enumerate(projections):
+            if i == V:
+                load_x(1)
             load_bias(i)
             by_quadrant = proj["scales"].rearrange("g (q r) n -> q r g n", r=SCALE_ROWS)
             for quadrant in range(QUADRANTS):
@@ -120,7 +124,7 @@ def tile_knnxlmultiheadsattention_pa_kernel(
                     in_=by_quadrant[quadrant].bitcast(I32),
                 )
             words = proj["words"].rearrange("g p n t -> p g (n t)").bitcast(I32)
-            if i == V:
+            if i != K:
                 for nb in range(BANKS_PER_ROW):
                     cols = slice(BANK * nb, BANK * (nb + 1))
                     nc.sync.dma_start(out=w_codes[:, i, :, cols], in_=words[:, :, cols])
@@ -130,7 +134,7 @@ def tile_knnxlmultiheadsattention_pa_kernel(
 
         x_words = x_sb[:].bitcast(F32)
 
-        def turn_x(j):
+        def turn_x(j, copy):
             flipped = psum.tile([P, PASSES, 2, P], F32, tag="bank")
             for g in range(PASSES):
                 for u in range(2):
@@ -139,7 +143,7 @@ def tile_knnxlmultiheadsattention_pa_kernel(
                         x_words[:, j, WORDS_PER_PASS * g + u : WORDS_PER_PASS * (g + 1) : 2],
                         identity[:],
                     )
-            nc.scalar.copy(
+            copy(
                 out=x_grouped[:, j, :].bitcast(F32).rearrange("p (g r u) -> p g r u", g=PASSES, u=2),
                 in_=flipped[:].rearrange("p g u r -> p g r u"),
             )
@@ -200,6 +204,13 @@ def tile_knnxlmultiheadsattention_pa_kernel(
                 out=squares[:, heads, :], in_=y_all[:, i, heads, j, :], func=ACT.Square, accum_out=total
             )
 
+        def square_sum_on_vector(i, j, total):
+            squares = small.tile([P, HEADS, HEAD_DIM], F32)
+            y = y_all[:, i, :, j, :]
+            nc.vector.scalar_tensor_tensor(
+                out=squares[:], in0=y, scalar=1.0, in1=y, op0=ALU.mult, op1=ALU.mult, accum_out=total
+            )
+
         def invert_norms(excess):
             inverse = small.tile([P, PAIR], F32)
             nc.scalar.activation(
@@ -209,25 +220,29 @@ def tile_knnxlmultiheadsattention_pa_kernel(
 
         def scale(i, pair, inverse):
             for heads in head_groups:
+                y = y_all[:, i, heads, PAIR * pair, :]
+                nc.gpsimd.tensor_scalar(
+                    out=y, in0=y, scalar1=inverse[:, 0:1], scalar2=0.0, op0=ALU.mult, op1=ALU.add
+                )
+                y = y_all[:, i, heads, PAIR * pair + 1, :]
+                nc.scalar.activation(out=y, in_=y, func=ACT.Copy, scale=inverse[:, 1:2])
+
+        def scale_on_vector(i, pair, inverse):
+            for heads in head_groups:
                 for n in range(PAIR):
                     y = y_all[:, i, heads, PAIR * pair + n, :]
-                    nc.gpsimd.tensor_scalar(
-                        out=y,
-                        in0=y,
-                        scalar1=inverse[:, n : n + 1],
-                        scalar2=0.0,
-                        op0=ALU.mult,
-                        op1=ALU.add,
+                    nc.vector.tensor_scalar(
+                        out=y, in0=y, scalar1=inverse[:, n : n + 1], scalar2=None, op0=ALU.mult
                     )
 
-        def first_normalised_pair(i):
+        def multiply_pair_by_banks(i, pair):
             halves = [small.tile([P, PAIR], F32, name="half%d" % nb) for nb in range(BANKS_PER_ROW)]
             lowered = small.tile([P, PAIR], F32)
             excess = small.tile([P, PAIR], F32)
             for nb in range(BANKS_PER_ROW):
                 for n in range(PAIR):
-                    multiply_and_add_bias(i, n, [nb])
-                    square_sum(i, n, head_groups[nb], halves[nb][:, n : n + 1])
+                    multiply_and_add_bias(i, PAIR * pair + n, [nb])
+                    square_sum(i, PAIR * pair + n, head_groups[nb], halves[nb][:, n : n + 1])
                 if nb == 0:
                     nc.scalar.activation(
                         out=lowered[:], in_=halves[0][:], func=ACT.Identity, bias=-NORM_FLOOR_SQUARED
@@ -239,21 +254,25 @@ def tile_knnxlmultiheadsattention_pa_kernel(
                     func=ACT.Relu,
                     bias=lowered[:, n : n + 1],
                 )
-            scale(i, 0, invert_norms(excess))
+            return invert_norms(excess)
 
-        def normalised_pair(i, pair):
+        def multiply_pair(i, pair, last=False):
             sums = small.tile([P, PAIR], F32)
             excess = small.tile([P, PAIR], F32)
             for n in range(PAIR):
-                multiply_and_add_bias(i, PAIR * pair + n, range(BANKS_PER_ROW))
-                square_sum(i, PAIR * pair + n, slice(0, HEADS), sums[:, n : n + 1])
+                j = PAIR * pair + n
+                multiply_and_add_bias(i, j, range(BANKS_PER_ROW))
+                if last and n == PAIR - 1:
+                    square_sum_on_vector(i, j, sums[:, n : n + 1])
+                else:
+                    square_sum(i, j, slice(0, HEADS), sums[:, n : n + 1])
             nc.scalar.activation(
                 out=excess[:], in_=sums[:], func=ACT.Relu, bias=-NORM_FLOOR_SQUARED
             )
-            scale(i, pair, invert_norms(excess))
+            return invert_norms(excess)
 
-        def store(i, tiles):
-            for heads in head_groups:
+        def store(i, tiles, groups=head_groups):
+            for heads in groups:
                 for b in range(BATCH):
                     out = projections[i]["out"][b][heads].rearrange(
                         "h (c j) d -> c h j d", j=TOKEN_TILES
@@ -263,23 +282,33 @@ def tile_knnxlmultiheadsattention_pa_kernel(
                         in_=y_all[b:P:BATCH, i, heads, tiles, :].rearrange("p h j d -> p h (j d)"),
                     )
 
-        for j in range(TOKEN_TILES):
-            turn_x(j)
+        for j in range(PAIR):
+            turn_x(j, nc.scalar.copy)
             quantise_x(j)
+        spread_bias(Q, nc.scalar.copy)
+        inverse = multiply_pair_by_banks(Q, 0)
+        for j in range(PAIR, TOKEN_TILES):
+            turn_x(j, nc.vector.tensor_copy)
+        for j in range(PAIR, TOKEN_TILES):
+            quantise_x(j)
+        spread_bias(V, nc.scalar.copy)
+        scale(Q, 0, inverse)
+        for j in range(TOKEN_TILES - 1):
+            multiply_and_add_bias(V, j, [0])
+        multiply_then_add_bias(V, TOKEN_TILES - 1, 0)
+        scale(Q, 1, multiply_pair(Q, 1))
+        for j in range(TOKEN_TILES):
+            multiply_and_add_bias(V, j, [1])
             if j == PAIR - 1:
-                spread_bias(V, nc.scalar.copy)
-        for nb in range(BANKS_PER_ROW):
-            for j in range(TOKEN_TILES - 1):
-                multiply_and_add_bias(V, j, [nb])
-                if nb == 0 and j == PAIR - 1:
-                    spread_bias(Q, nc.scalar.copy)
-            multiply_then_add_bias(V, TOKEN_TILES - 1, nb)
-        first_normalised_pair(Q)
-        normalised_pair(Q, 1)
-        spread_bias(K, nc.vector.tensor_copy)
-        normalised_pair(K, 0)
-        normalised_pair(K, 1)
-        store(V, slice(0, TOKEN_TILES))
-        for i in (Q, K):
-            for pair in range(TOKEN_TILES // PAIR):
-                store(i, slice(PAIR * pair, PAIR * (pair + 1)))
+                spread_bias(K, nc.vector.tensor_copy)
+        scale(K, 0, multiply_pair(K, 0))
+        scale_on_vector(K, 1, multiply_pair(K, 1, last=True))
+
+        first_pair, second_pair = slice(0, PAIR), slice(PAIR, TOKEN_TILES)
+        all_tiles = slice(0, TOKEN_TILES)
+        store(Q, first_pair)
+        store(V, all_tiles, head_groups[:1])
+        store(Q, second_pair)
+        store(V, all_tiles, head_groups[1:])
+        store(K, first_pair)
+        store(K, second_pair)

@@ -31,7 +31,7 @@ QUADRANTS = 4
 PAIR = 2
 NORM_FLOOR_SQUARED = 1e-24
 
-IDLE_MATMULS = 4
+IDLE_MATMULS = 14
 
 FLOPS = 2 * BATCH * SEQ * EMBED * 3 * FEATURES
 
@@ -82,19 +82,27 @@ def tile_knnxlmultiheadsattention_pa_kernel(
         ones = keep.tile([P, P], BF16)
         identity = keep.tile([P, P], F32)
         table_warmer = keep.tile([P, 2], F32)
-        idle_rhs = keep.tile([P, BANK], BF16)
 
-        for i in range(count):
+        def zero_scales(engine, i):
+            engine.memset(w_scales[:, i, :, :].rearrange("p g n -> p (g n)").bitcast(I32), 0)
+
+        zero_scales(nc.gpsimd, Q)
+        nc.vector.memset(ones[:], 1.0)
+        nc.vector.memset(bias_rows[:, Q, :].bitcast(I32), 0)
+        nc.vector.memset(table_warmer[:], 1.0)
+        for i in (V, K):
             nc.vector.memset(bias_rows[:, i, :].bitcast(I32), 0)
-            nc.vector.memset(w_scales[:, i, :, :].rearrange("p g n -> p (g n)").bitcast(I32), 0)
-            if i == Q:
-                nc.vector.memset(ones[:], 1.0)
-                nc.vector.memset(idle_rhs[:], 0.0)
-                nc.vector.memset(table_warmer[:], 1.0)
+            zero_scales(nc.vector, i)
         make_identity(nc, identity[:])
         idle_bank = psum.tile([P, BANK], F32, tag="bank")
         for n in range(IDLE_MATMULS):
-            nc.tensor.matmul(out=idle_bank[:], lhsT=ones[:], rhs=idle_rhs[:], start=True, stop=True)
+            nc.tensor.matmul(
+                out=idle_bank[:, :P],
+                lhsT=ones[:],
+                rhs=ones[:],
+                start=True,
+                stop=True,
+            )
         nc.scalar.activation(
             out=table_warmer[:, 1:2], in_=table_warmer[:, 0:1], func=ACT.Abs_reciprocal_sqrt
         )
@@ -189,15 +197,6 @@ def tile_knnxlmultiheadsattention_pa_kernel(
                     op=ALU.add,
                 )
 
-        def multiply_then_add_bias(i, j, nb):
-            cols = slice(BANK * nb, BANK * (nb + 1))
-            acc = multiply(i, j, [nb])[0]
-            y = y_all[:, i, head_groups[nb], j, :]
-            nc.scalar.copy(out=y, in_=acc[:].rearrange("p (h d) -> p h d", d=HEAD_DIM))
-            nc.gpsimd.tensor_tensor(
-                out=y, in0=y, in1=bias_all[:, i, cols].rearrange("p (h d) -> p h d", d=HEAD_DIM), op=ALU.add
-            )
-
         def square_sum(i, j, heads, total):
             squares = small.tile([P, HEADS, HEAD_DIM], F32)
             nc.scalar.activation(
@@ -235,7 +234,7 @@ def tile_knnxlmultiheadsattention_pa_kernel(
                         out=y, in0=y, scalar1=inverse[:, n : n + 1], scalar2=None, op0=ALU.mult
                     )
 
-        def multiply_pair_by_banks(i, pair):
+        def multiply_pair(i, pair):
             halves = [small.tile([P, PAIR], F32, name="half%d" % nb) for nb in range(BANKS_PER_ROW)]
             lowered = small.tile([P, PAIR], F32)
             excess = small.tile([P, PAIR], F32)
@@ -244,8 +243,12 @@ def tile_knnxlmultiheadsattention_pa_kernel(
                     multiply_and_add_bias(i, PAIR * pair + n, [nb])
                     square_sum(i, PAIR * pair + n, head_groups[nb], halves[nb][:, n : n + 1])
                 if nb == 0:
-                    nc.scalar.activation(
-                        out=lowered[:], in_=halves[0][:], func=ACT.Identity, bias=-NORM_FLOOR_SQUARED
+                    nc.gpsimd.tensor_scalar(
+                        out=lowered[:],
+                        in0=halves[0][:],
+                        scalar1=-NORM_FLOOR_SQUARED,
+                        scalar2=None,
+                        op0=ALU.add,
                     )
             for n in range(PAIR):
                 nc.scalar.activation(
@@ -256,13 +259,13 @@ def tile_knnxlmultiheadsattention_pa_kernel(
                 )
             return invert_norms(excess)
 
-        def multiply_pair(i, pair, last=False):
+        def multiply_last_pair(i, pair):
             sums = small.tile([P, PAIR], F32)
             excess = small.tile([P, PAIR], F32)
             for n in range(PAIR):
                 j = PAIR * pair + n
                 multiply_and_add_bias(i, j, range(BANKS_PER_ROW))
-                if last and n == PAIR - 1:
+                if n == PAIR - 1:
                     square_sum_on_vector(i, j, sums[:, n : n + 1])
                 else:
                     square_sum(i, j, slice(0, HEADS), sums[:, n : n + 1])
@@ -286,29 +289,27 @@ def tile_knnxlmultiheadsattention_pa_kernel(
             turn_x(j, nc.scalar.copy)
             quantise_x(j)
         spread_bias(Q, nc.scalar.copy)
-        inverse = multiply_pair_by_banks(Q, 0)
+        inverse = multiply_pair(Q, 0)
         for j in range(PAIR, TOKEN_TILES):
             turn_x(j, nc.vector.tensor_copy)
         for j in range(PAIR, TOKEN_TILES):
             quantise_x(j)
         spread_bias(V, nc.scalar.copy)
         scale(Q, 0, inverse)
-        for j in range(TOKEN_TILES - 1):
+        for j in range(TOKEN_TILES):
             multiply_and_add_bias(V, j, [0])
-        multiply_then_add_bias(V, TOKEN_TILES - 1, 0)
+        spread_bias(K, nc.scalar.copy)
         scale(Q, 1, multiply_pair(Q, 1))
         for j in range(TOKEN_TILES):
             multiply_and_add_bias(V, j, [1])
-            if j == PAIR - 1:
-                spread_bias(K, nc.vector.tensor_copy)
         scale(K, 0, multiply_pair(K, 0))
-        scale_on_vector(K, 1, multiply_pair(K, 1, last=True))
+        scale_on_vector(K, 1, multiply_last_pair(K, 1))
 
         first_pair, second_pair = slice(0, PAIR), slice(PAIR, TOKEN_TILES)
         all_tiles = slice(0, TOKEN_TILES)
         store(Q, first_pair)
         store(V, all_tiles, head_groups[:1])
-        store(Q, second_pair)
         store(V, all_tiles, head_groups[1:])
+        store(Q, second_pair)
         store(K, first_pair)
         store(K, second_pair)

@@ -116,7 +116,7 @@ def tile_knnxlmultiheadsattention_pa_kernel(
             tiles = slice(PAIR * pair, PAIR * (pair + 1))
             nc.sync.dma_start(
                 out=x_sb[:, tiles, :].rearrange("p j e -> p (j e)"),
-                in_=x.rearrange("b (c h j) e -> h c b (j e)", h=TOKEN_TILES // PAIR, j=PAIR)[pair],
+                in_=x[pair].rearrange("(c j) e -> c (j e)", j=PAIR),
             )
 
         load_x(0)
@@ -274,16 +274,13 @@ def tile_knnxlmultiheadsattention_pa_kernel(
             )
             return invert_norms(excess)
 
-        def store(i, tiles, groups=head_groups):
+        def store(i, pair, groups=head_groups):
+            tiles = slice(PAIR * pair, PAIR * (pair + 1))
             for heads in groups:
-                for b in range(BATCH):
-                    out = projections[i]["out"][b][heads].rearrange(
-                        "h (c j) d -> c h j d", j=TOKEN_TILES
-                    )
-                    nc.sync.dma_start(
-                        out=out[:, :, tiles, :].rearrange("c h j d -> c h (j d)"),
-                        in_=y_all[b:P:BATCH, i, heads, tiles, :].rearrange("p h j d -> p h (j d)"),
-                    )
+                nc.sync.dma_start(
+                    out=projections[i]["out"][pair][heads].rearrange("h (c j) d -> c h (j d)", j=PAIR),
+                    in_=y_all[:, i, heads, tiles, :].rearrange("p h j d -> p h (j d)"),
+                )
 
         for j in range(PAIR):
             turn_x(j, nc.scalar.copy)
@@ -305,11 +302,10 @@ def tile_knnxlmultiheadsattention_pa_kernel(
         scale(K, 0, multiply_pair(K, 0))
         scale_on_vector(K, 1, multiply_last_pair(K, 1))
 
-        first_pair, second_pair = slice(0, PAIR), slice(PAIR, TOKEN_TILES)
-        all_tiles = slice(0, TOKEN_TILES)
-        store(Q, first_pair)
-        store(V, all_tiles, head_groups[:1])
-        store(V, all_tiles, head_groups[1:])
-        store(Q, second_pair)
-        store(K, first_pair)
-        store(K, second_pair)
+        store(Q, 0)
+        for heads in head_groups:
+            for pair in range(BATCH):
+                store(V, pair, [heads])
+        store(Q, 1)
+        store(K, 0)
+        store(K, 1)

@@ -31,7 +31,7 @@ QUADRANTS = 4
 PAIR = 2
 NORM_FLOOR_SQUARED = 1e-24
 
-IDLE_MATMULS = 14
+IDLE_MATMULS = 20
 
 FLOPS = 2 * BATCH * SEQ * EMBED * 3 * FEATURES
 
@@ -86,8 +86,8 @@ def tile_knnxlmultiheadsattention_pa_kernel(
         def zero_scales(engine, i):
             engine.memset(w_scales[:, i, :, :].rearrange("p g n -> p (g n)").bitcast(I32), 0)
 
+        nc.gpsimd.memset(ones[:], 1.0)
         zero_scales(nc.gpsimd, Q)
-        nc.vector.memset(ones[:], 1.0)
         nc.vector.memset(bias_rows[:, Q, :].bitcast(I32), 0)
         nc.vector.memset(table_warmer[:], 1.0)
         for i in (V, K):
@@ -103,14 +103,14 @@ def tile_knnxlmultiheadsattention_pa_kernel(
                 start=True,
                 stop=True,
             )
-        nc.scalar.activation(
-            out=table_warmer[:, 1:2], in_=table_warmer[:, 0:1], func=ACT.Abs_reciprocal_sqrt
-        )
-
         def load_bias(i):
             nc.sync.dma_start(
                 out=bias_rows[0:1, i, :], in_=projections[i]["bias"].rearrange("(o n) -> o n", o=1)
             )
+
+        nc.scalar.activation(
+            out=table_warmer[:, 1:2], in_=table_warmer[:, 0:1], func=ACT.Abs_reciprocal_sqrt
+        )
 
         def load_x(pair):
             tiles = slice(PAIR * pair, PAIR * (pair + 1))
@@ -142,23 +142,31 @@ def tile_knnxlmultiheadsattention_pa_kernel(
 
         x_words = x_sb[:].bitcast(F32)
 
-        def turn_x(j, copy):
-            flipped = psum.tile([P, PASSES, 2, P], F32, tag="bank")
-            for g in range(PASSES):
+        def turn_x(j, passes, copy):
+            flipped = psum.tile([P, len(passes), 2, P], F32, tag="bank")
+            for n, g in enumerate(passes):
                 for u in range(2):
                     nc.tensor.transpose(
-                        flipped[:, g, u, :],
+                        flipped[:, n, u, :],
                         x_words[:, j, WORDS_PER_PASS * g + u : WORDS_PER_PASS * (g + 1) : 2],
                         identity[:],
                     )
             copy(
-                out=x_grouped[:, j, :].bitcast(F32).rearrange("p (g r u) -> p g r u", g=PASSES, u=2),
+                out=x_grouped[:, j, pass_columns(passes, 4 * P)]
+                .bitcast(F32)
+                .rearrange("p (g r u) -> p g r u", g=len(passes), u=2),
                 in_=flipped[:].rearrange("p g u r -> p g r u"),
             )
 
-        def quantise_x(j):
+        def pass_columns(passes, width):
+            return slice(width * passes[0], width * (passes[-1] + 1))
+
+        def quantise_x(j, passes):
+            columns = pass_columns(passes, P)
             nc.vector.quantize_mx(
-                out=x_codes[:, j, :].bitcast(FP8X4), scales=x_scales[:, j, :], in_=x_grouped[:, j, :]
+                out=x_codes[:, j, columns].bitcast(FP8X4),
+                scales=x_scales[:, j, columns],
+                in_=x_grouped[:, j, pass_columns(passes, 4 * P)],
             )
 
         def spread_bias(i, copy):
@@ -197,6 +205,15 @@ def tile_knnxlmultiheadsattention_pa_kernel(
                     op=ALU.add,
                 )
 
+        def multiply_then_add_bias(i, j, nb):
+            cols = slice(BANK * nb, BANK * (nb + 1))
+            acc = multiply(i, j, [nb])[0]
+            y = y_all[:, i, head_groups[nb], j, :]
+            nc.scalar.copy(out=y, in_=acc[:].rearrange("p (h d) -> p h d", d=HEAD_DIM))
+            nc.gpsimd.tensor_tensor(
+                out=y, in0=y, in1=bias_all[:, i, cols].rearrange("p (h d) -> p h d", d=HEAD_DIM), op=ALU.add
+            )
+
         def square_sum(i, j, heads, total):
             squares = small.tile([P, HEADS, HEAD_DIM], F32)
             nc.scalar.activation(
@@ -225,6 +242,14 @@ def tile_knnxlmultiheadsattention_pa_kernel(
                 )
                 y = y_all[:, i, heads, PAIR * pair + 1, :]
                 nc.scalar.activation(out=y, in_=y, func=ACT.Copy, scale=inverse[:, 1:2])
+
+        def scale_on_gpsimd(i, pair, inverse):
+            for n, groups in enumerate([[slice(0, HEADS)], head_groups]):
+                for heads in groups:
+                    y = y_all[:, i, heads, PAIR * pair + n, :]
+                    nc.gpsimd.tensor_scalar(
+                        out=y, in0=y, scalar1=inverse[:, n : n + 1], scalar2=0.0, op0=ALU.mult, op1=ALU.add
+                    )
 
         def scale_on_vector(i, pair, inverse):
             for heads in head_groups:
@@ -283,20 +308,25 @@ def tile_knnxlmultiheadsattention_pa_kernel(
                 )
 
         for j in range(PAIR):
-            turn_x(j, nc.scalar.copy)
-            quantise_x(j)
+            for g in range(PASSES):
+                turn_x(j, [g], nc.scalar.copy)
+                quantise_x(j, [g])
         spread_bias(Q, nc.scalar.copy)
         inverse = multiply_pair(Q, 0)
+        both = list(range(PASSES))
         for j in range(PAIR, TOKEN_TILES):
-            turn_x(j, nc.vector.tensor_copy)
+            turn_x(j, both, nc.vector.tensor_copy)
         for j in range(PAIR, TOKEN_TILES):
-            quantise_x(j)
-        spread_bias(V, nc.scalar.copy)
+            quantise_x(j, both)
+        spread_bias(V, nc.vector.tensor_copy)
         scale(Q, 0, inverse)
         for j in range(TOKEN_TILES):
-            multiply_and_add_bias(V, j, [0])
+            if j == 3:
+                multiply_then_add_bias(V, j, 0)
+            else:
+                multiply_and_add_bias(V, j, [0])
         spread_bias(K, nc.scalar.copy)
-        scale(Q, 1, multiply_pair(Q, 1))
+        scale_on_gpsimd(Q, 1, multiply_pair(Q, 1))
         for j in range(TOKEN_TILES):
             multiply_and_add_bias(V, j, [1])
         scale(K, 0, multiply_pair(K, 0))

@@ -77,12 +77,17 @@ def tile_knnxlmultiheadsattention_pa_kernel(
         w_codes = keep.tile([P, count, PASSES, FEATURES], I32, align_bytes=64)
         w_scales = keep.tile([P, count, PASSES, FEATURES], U8, align_bytes=64)
         bias_rows = keep.tile([P, count, FEATURES], BF16)
+        bias_in = keep.tile([P, FEATURES], BF16)
         bias_all = keep.tile([P, count, FEATURES], BF16)
         y_all = keep.tile([P, count, HEADS, TOKEN_TILES, HEAD_DIM], F32)
         ones = keep.tile([P, P], BF16)
         identity = keep.tile([P, P], F32)
         table_warmer = keep.tile([P, 2], F32)
 
+        def load_bias(queue, i, row):
+            queue.dma_start(out=row, in_=projections[i]["bias"].rearrange("(o n) -> o n", o=1))
+
+        load_bias(nc.sync, Q, bias_in[0:1, :])
         def zero_scales(engine, i):
             engine.memset(w_scales[:, i, :, :].rearrange("p g n -> p (g n)").bitcast(I32), 0)
 
@@ -93,7 +98,10 @@ def tile_knnxlmultiheadsattention_pa_kernel(
         for i in (V, K):
             nc.vector.memset(bias_rows[:, i, :].bitcast(I32), 0)
             zero_scales(nc.vector, i)
+        nc.vector.tensor_copy(out=bias_rows[0:1, Q, :], in_=bias_in[0:1, :])
         make_identity(nc, identity[:])
+        for i in (V, K):
+            load_bias(nc.gpsimd, i, bias_rows[0:1, i, :])
         idle_bank = psum.tile([P, BANK], F32, tag="bank")
         for n in range(IDLE_MATMULS):
             nc.tensor.matmul(
@@ -103,11 +111,6 @@ def tile_knnxlmultiheadsattention_pa_kernel(
                 start=True,
                 stop=True,
             )
-        def load_bias(i):
-            nc.sync.dma_start(
-                out=bias_rows[0:1, i, :], in_=projections[i]["bias"].rearrange("(o n) -> o n", o=1)
-            )
-
         nc.scalar.activation(
             out=table_warmer[:, 1:2], in_=table_warmer[:, 0:1], func=ACT.Abs_reciprocal_sqrt
         )
@@ -119,11 +122,13 @@ def tile_knnxlmultiheadsattention_pa_kernel(
                 in_=x[pair].rearrange("(c j) e -> c (j e)", j=PAIR),
             )
 
-        load_x(0)
+        for j in range(PAIR):
+            nc.sync.dma_start(
+                out=x_sb[:, j, :], in_=x[0].rearrange("(c j) e -> j c e", j=PAIR)[j]
+            )
         for i, proj in enumerate(projections):
             if i == V:
                 load_x(1)
-            load_bias(i)
             by_quadrant = proj["scales"].rearrange("g (q r) n -> q r g n", r=SCALE_ROWS)
             for quadrant in range(QUADRANTS):
                 first = 32 * quadrant + SCALE_ROWS * i
@@ -290,7 +295,7 @@ def tile_knnxlmultiheadsattention_pa_kernel(
             for n in range(PAIR):
                 j = PAIR * pair + n
                 multiply_and_add_bias(i, j, range(BANKS_PER_ROW))
-                if n == PAIR - 1:
+                if n == PAIR - 1 and True:
                     square_sum_on_vector(i, j, sums[:, n : n + 1])
                 else:
                     square_sum(i, j, slice(0, HEADS), sums[:, n : n + 1])
@@ -298,6 +303,19 @@ def tile_knnxlmultiheadsattention_pa_kernel(
                 out=excess[:], in_=sums[:], func=ACT.Relu, bias=-NORM_FLOOR_SQUARED
             )
             return invert_norms(excess)
+
+        def scale_mixed(i, pair, inverse, how):
+            for word in how.split():
+                n, who = int(word[0]), word[2]
+                heads = slice(0, HEADS) if word[1] == "*" else head_groups[int(word[1])]
+                y = y_all[:, i, heads, PAIR * pair + n, :]
+                factor = inverse[:, n : n + 1]
+                if who == "G":
+                    nc.gpsimd.tensor_scalar(out=y, in0=y, scalar1=factor, scalar2=0.0, op0=ALU.mult, op1=ALU.add)
+                elif who == "S":
+                    nc.scalar.activation(out=y, in_=y, func=ACT.Copy, scale=factor)
+                else:
+                    nc.vector.tensor_scalar(out=y, in0=y, scalar1=factor, scalar2=None, op0=ALU.mult)
 
         def store(i, pair, groups=head_groups):
             tiles = slice(PAIR * pair, PAIR * (pair + 1))
@@ -319,23 +337,25 @@ def tile_knnxlmultiheadsattention_pa_kernel(
         for j in range(PAIR, TOKEN_TILES):
             quantise_x(j, both)
         spread_bias(V, nc.vector.tensor_copy)
-        scale(Q, 0, inverse)
-        for j in range(TOKEN_TILES):
-            if j == 3:
-                multiply_then_add_bias(V, j, 0)
-            else:
-                multiply_and_add_bias(V, j, [0])
+        scale_mixed(Q, 0, inverse, "00G 10S 01G 11S")
+        multiply_and_add_bias(V, 0, [0])
+        multiply_and_add_bias(V, 1, [0])
+        multiply_and_add_bias(V, 2, [0])
+        multiply_then_add_bias(V, 3, 0)
         spread_bias(K, nc.scalar.copy)
-        scale_on_gpsimd(Q, 1, multiply_pair(Q, 1))
-        for j in range(TOKEN_TILES):
-            multiply_and_add_bias(V, j, [1])
-        scale(K, 0, multiply_pair(K, 0))
-        scale_on_vector(K, 1, multiply_last_pair(K, 1))
+        scale_mixed(Q, 1, multiply_pair(Q, 1), "0*G 10G 11G")
+        multiply_and_add_bias(V, 0, [1])
+        multiply_and_add_bias(V, 1, [1])
+        multiply_and_add_bias(V, 2, [1])
+        multiply_and_add_bias(V, 3, [1])
+        scale_mixed(K, 0, multiply_pair(K, 0), "00G 10S 01G 11S")
+        scale_mixed(K, 1, multiply_last_pair(K, 1), "00V 10S 01V 11S")
 
         store(Q, 0)
-        for heads in head_groups:
-            for pair in range(BATCH):
-                store(V, pair, [heads])
+        store(V, 0, [head_groups[0]])
+        store(V, 1, [head_groups[0]])
+        store(V, 0, [head_groups[1]])
+        store(V, 1, [head_groups[1]])
         store(Q, 1)
         store(K, 0)
         store(K, 1)

@@ -307,7 +307,7 @@ def tile_knnxlmultiheadsattention_pa_kernel(
         def scale_mixed(i, pair, inverse, how):
             for word in how.split():
                 n, who = int(word[0]), word[2]
-                heads = slice(0, HEADS) if word[1] == "*" else head_groups[int(word[1])]
+                heads = slice(0, HEADS) if word[1] == "*" else head_groups[int(word[1])] if word[1] in "01" else slice(2 * "abcd".index(word[1]), 2 * "abcd".index(word[1]) + 2)
                 y = y_all[:, i, heads, PAIR * pair + n, :]
                 factor = inverse[:, n : n + 1]
                 if who == "G":
@@ -349,7 +349,7 @@ def tile_knnxlmultiheadsattention_pa_kernel(
         multiply_and_add_bias(V, 2, [1])
         multiply_and_add_bias(V, 3, [1])
         scale_mixed(K, 0, multiply_pair(K, 0), "00G 10S 01G 11S")
-        scale_mixed(K, 1, multiply_last_pair(K, 1), "00V 10S 01V 11S")
+        scale_mixed(K, 1, multiply_last_pair(K, 1), "0aV 1aS 0bV 1bS 01V 11S")
 
         store(Q, 0)
         store(V, 0, [head_groups[0]])
@@ -358,4 +358,4 @@ def tile_knnxlmultiheadsattention_pa_kernel(
         store(V, 1, [head_groups[1]])
         store(Q, 1)
         store(K, 0)
-        store(K, 1)
+        store(K, 1, [slice(0, 2), slice(2, 4), head_groups[1]])

from contextlib import ExitStack

import concourse.mybir as mybir
from concourse.masks import make_identity

F32 = mybir.dt.float32
BF16 = mybir.dt.bfloat16
I32 = mybir.dt.int32
U32 = mybir.dt.uint32
U8 = mybir.dt.uint8
FP8X4 = mybir.dt.float8_e4m3fn_x4
ALU = mybir.AluOpType
ACT = mybir.ActivationFunctionType

P = 128
BATCH = 2
SEQ = 256
EMBED = 1024
FEATURES = 1024
HEADS = 8
HEAD_DIM = 128
TOKEN_TILES = BATCH * SEQ // P
K_PASS = 4 * P
PASSES = EMBED // K_PASS
BANK = 512
BANKS_PER_ROW = FEATURES // BANK
HEADS_PER_BANK = BANK // HEAD_DIM
WORDS_PER_PASS = K_PASS // 2
SCALE_ROWS = 4
QUADRANTS = 4
PAIR = 2
NORM_FLOOR_SQUARED = 1e-24

IDLE_MATMULS = 20

FLOPS = 2 * BATCH * SEQ * EMBED * 3 * FEATURES


def tile_knnxlmultiheadsattention_pa_kernel(
    tc,
    x,
    wq_words,
    wq_scales,
    bq,
    wk_words,
    wk_scales,
    bk,
    wv_words,
    wv_scales,
    bv,
    out_q,
    out_k,
    out_v,
):
    nc = tc.nc
    projections = [
        dict(words=wq_words, scales=wq_scales, bias=bq, out=out_q),
        dict(words=wv_words, scales=wv_scales, bias=bv, out=out_v),
        dict(words=wk_words, scales=wk_scales, bias=bk, out=out_k),
    ]
    Q, V, K = range(len(projections))
    count = len(projections)
    head_groups = [
        slice(HEADS_PER_BANK * nb, HEADS_PER_BANK * (nb + 1)) for nb in range(BANKS_PER_ROW)
    ]

    with ExitStack() as stack:
        keep = stack.enter_context(tc.tile_pool(name="keep", bufs=1))
        small = stack.enter_context(tc.tile_pool(name="small", bufs=4))
        psum = stack.enter_context(tc.psum_pool(name="psum", bufs=8))
        stack.enter_context(tc.manual_schedule())

        x_sb = keep.tile([P, TOKEN_TILES, EMBED], BF16)
        x_grouped = keep.tile([P, TOKEN_TILES, PASSES * P * 4], BF16, align_bytes=64)
        x_codes = keep.tile([P, TOKEN_TILES, PASSES * P], U32, align_bytes=64)
        x_scales = keep.tile([P, TOKEN_TILES, PASSES * P], U8, align_bytes=64)
        w_codes = keep.tile([P, count, PASSES, FEATURES], I32, align_bytes=64)
        w_scales = keep.tile([P, count, PASSES, FEATURES], U8, align_bytes=64)
        bias_rows = keep.tile([P, count, FEATURES], BF16)
        bias_in = keep.tile([P, FEATURES], BF16)
        bias_all = keep.tile([P, count, FEATURES], BF16)
        y_all = keep.tile([P, count, HEADS, TOKEN_TILES, HEAD_DIM], F32)
        ones = keep.tile([P, P], BF16)
        identity = keep.tile([P, P], F32)
        table_warmer = keep.tile([P, 2], F32)

        def load_bias(queue, i, row):
            queue.dma_start(out=row, in_=projections[i]["bias"].rearrange("(o n) -> o n", o=1))

        load_bias(nc.sync, Q, bias_in[0:1, :])
        def zero_scales(engine, i):
            engine.memset(w_scales[:, i, :, :].rearrange("p g n -> p (g n)").bitcast(I32), 0)

        nc.gpsimd.memset(ones[:], 1.0)
        zero_scales(nc.gpsimd, Q)
        nc.vector.memset(bias_rows[:, Q, :].bitcast(I32), 0)
        nc.vector.memset(table_warmer[:], 1.0)
        for i in (V, K):
            nc.vector.memset(bias_rows[:, i, :].bitcast(I32), 0)
            zero_scales(nc.vector, i)
        nc.vector.tensor_copy(out=bias_rows[0:1, Q, :], in_=bias_in[0:1, :])
        make_identity(nc, identity[:])
        for i in (V, K):
            load_bias(nc.gpsimd, i, bias_rows[0:1, i, :])
        idle_bank = psum.tile([P, BANK], F32, tag="bank")
        for n in range(IDLE_MATMULS):
            nc.tensor.matmul(
                out=idle_bank[:, :P],
                lhsT=ones[:],
                rhs=ones[:],
                start=True,
                stop=True,
            )
        nc.scalar.activation(
            out=table_warmer[:, 1:2], in_=table_warmer[:, 0:1], func=ACT.Abs_reciprocal_sqrt
        )

        def load_x(pair):
            tiles = slice(PAIR * pair, PAIR * (pair + 1))
            nc.sync.dma_start(
                out=x_sb[:, tiles, :].rearrange("p j e -> p (j e)"),
                in_=x[pair].rearrange("(c j) e -> c (j e)", j=PAIR),
            )

        for j in range(PAIR):
            nc.sync.dma_start(
                out=x_sb[:, j, :], in_=x[0].rearrange("(c j) e -> j c e", j=PAIR)[j]
            )
        for i, proj in enumerate(projections):
            if i == V:
                load_x(1)
            by_quadrant = proj["scales"].rearrange("g (q r) n -> q r g n", r=SCALE_ROWS)
            for quadrant in range(QUADRANTS):
                first = 32 * quadrant + SCALE_ROWS * i
                nc.sync.dma_start(
                    out=w_scales[first : first + SCALE_ROWS, i, :, :].bitcast(I32),
                    in_=by_quadrant[quadrant].bitcast(I32),
                )
            words = proj["words"].rearrange("g p n t -> p g (n t)").bitcast(I32)
            if i != K:
                for nb in range(BANKS_PER_ROW):
                    cols = slice(BANK * nb, BANK * (nb + 1))
                    nc.sync.dma_start(out=w_codes[:, i, :, cols], in_=words[:, :, cols])
            else:
                for g in range(PASSES):
                    nc.sync.dma_start(out=w_codes[:, i, g, :], in_=words[:, g, :])

        x_words = x_sb[:].bitcast(F32)

        def turn_x(j, passes, copy):
            flipped = psum.tile([P, len(passes), 2, P], F32, tag="bank")
            for n, g in enumerate(passes):
                for u in range(2):
                    nc.tensor.transpose(
                        flipped[:, n, u, :],
                        x_words[:, j, WORDS_PER_PASS * g + u : WORDS_PER_PASS * (g + 1) : 2],
                        identity[:],
                    )
            copy(
                out=x_grouped[:, j, pass_columns(passes, 4 * P)]
                .bitcast(F32)
                .rearrange("p (g r u) -> p g r u", g=len(passes), u=2),
                in_=flipped[:].rearrange("p g u r -> p g r u"),
            )

        def pass_columns(passes, width):
            return slice(width * passes[0], width * (passes[-1] + 1))

        def quantise_x(j, passes):
            columns = pass_columns(passes, P)
            nc.vector.quantize_mx(
                out=x_codes[:, j, columns].bitcast(FP8X4),
                scales=x_scales[:, j, columns],
                in_=x_grouped[:, j, pass_columns(passes, 4 * P)],
            )

        def spread_bias(i, copy):
            spread = psum.tile([P, FEATURES], BF16, tag="bank")
            for nb in range(BANKS_PER_ROW):
                cols = slice(BANK * nb, BANK * (nb + 1))
                nc.tensor.matmul(
                    out=spread[:, cols], lhsT=ones[:], rhs=bias_rows[:, i, cols], start=True, stop=True
                )
            copy(out=bias_all[:, i, :], in_=spread[:])

        def multiply(i, j, banks):
            accs = [psum.tile([P, BANK], F32, tag="bank", name="acc%d" % nb) for nb in banks]
            for g in range(PASSES):
                tokens = slice(P * g, P * (g + 1))
                for acc, nb in zip(accs, banks):
                    cols = slice(BANK * nb, BANK * (nb + 1))
                    nc.tensor.matmul_mx(
                        out=acc[:],
                        lhsT=x_codes[:, j, tokens].bitcast(FP8X4),
                        lhsT_scale=x_scales[:, j, tokens],
                        rhs=w_codes[:, i, g, cols].bitcast(FP8X4),
                        rhs_scale=w_scales[SCALE_ROWS * i : P, i, g, cols],
                        start=(g == 0),
                        stop=(g == PASSES - 1),
                    )
            return accs

        def multiply_and_add_bias(i, j, banks):
            for acc, nb in zip(multiply(i, j, banks), banks):
                cols = slice(BANK * nb, BANK * (nb + 1))
                nc.vector.tensor_tensor(
                    out=y_all[:, i, head_groups[nb], j, :],
                    in0=acc[:].rearrange("p (h d) -> p h d", d=HEAD_DIM),
                    in1=bias_all[:, i, cols].rearrange("p (h d) -> p h d", d=HEAD_DIM),
                    op=ALU.add,
                )

        def multiply_then_add_bias(i, j, nb):
            cols = slice(BANK * nb, BANK * (nb + 1))
            acc = multiply(i, j, [nb])[0]
            y = y_all[:, i, head_groups[nb], j, :]
            nc.scalar.copy(out=y, in_=acc[:].rearrange("p (h d) -> p h d", d=HEAD_DIM))
            nc.gpsimd.tensor_tensor(
                out=y, in0=y, in1=bias_all[:, i, cols].rearrange("p (h d) -> p h d", d=HEAD_DIM), op=ALU.add
            )

        def square_sum(i, j, heads, total):
            squares = small.tile([P, HEADS, HEAD_DIM], F32)
            nc.scalar.activation(
                out=squares[:, heads, :], in_=y_all[:, i, heads, j, :], func=ACT.Square, accum_out=total
            )

        def square_sum_on_vector(i, j, total):
            squares = small.tile([P, HEADS, HEAD_DIM], F32)
            y = y_all[:, i, :, j, :]
            nc.vector.scalar_tensor_tensor(
                out=squares[:], in0=y, scalar=1.0, in1=y, op0=ALU.mult, op1=ALU.mult, accum_out=total
            )

        def invert_norms(excess):
            inverse = small.tile([P, PAIR], F32)
            nc.scalar.activation(
                out=inverse[:], in_=excess[:], func=ACT.Abs_reciprocal_sqrt, bias=NORM_FLOOR_SQUARED
            )
            return inverse

        def scale(i, pair, inverse):
            for heads in head_groups:
                y = y_all[:, i, heads, PAIR * pair, :]
                nc.gpsimd.tensor_scalar(
                    out=y, in0=y, scalar1=inverse[:, 0:1], scalar2=0.0, op0=ALU.mult, op1=ALU.add
                )
                y = y_all[:, i, heads, PAIR * pair + 1, :]
                nc.scalar.activation(out=y, in_=y, func=ACT.Copy, scale=inverse[:, 1:2])

        def scale_on_gpsimd(i, pair, inverse):
            for n, groups in enumerate([[slice(0, HEADS)], head_groups]):
                for heads in groups:
                    y = y_all[:, i, heads, PAIR * pair + n, :]
                    nc.gpsimd.tensor_scalar(
                        out=y, in0=y, scalar1=inverse[:, n : n + 1], scalar2=0.0, op0=ALU.mult, op1=ALU.add
                    )

        def scale_on_vector(i, pair, inverse):
            for heads in head_groups:
                for n in range(PAIR):
                    y = y_all[:, i, heads, PAIR * pair + n, :]
                    nc.vector.tensor_scalar(
                        out=y, in0=y, scalar1=inverse[:, n : n + 1], scalar2=None, op0=ALU.mult
                    )

        def multiply_pair(i, pair):
            halves = [small.tile([P, PAIR], F32, name="half%d" % nb) for nb in range(BANKS_PER_ROW)]
            lowered = small.tile([P, PAIR], F32)
            excess = small.tile([P, PAIR], F32)
            for nb in range(BANKS_PER_ROW):
                for n in range(PAIR):
                    multiply_and_add_bias(i, PAIR * pair + n, [nb])
                    square_sum(i, PAIR * pair + n, head_groups[nb], halves[nb][:, n : n + 1])
                if nb == 0:
                    nc.gpsimd.tensor_scalar(
                        out=lowered[:],
                        in0=halves[0][:],
                        scalar1=-NORM_FLOOR_SQUARED,
                        scalar2=None,
                        op0=ALU.add,
                    )
            for n in range(PAIR):
                nc.scalar.activation(
                    out=excess[:, n : n + 1],
                    in_=halves[1][:, n : n + 1],
                    func=ACT.Relu,
                    bias=lowered[:, n : n + 1],
                )
            return invert_norms(excess)

        def multiply_last_pair(i, pair):
            sums = small.tile([P, PAIR], F32)
            excess = small.tile([P, PAIR], F32)
            for n in range(PAIR):
                j = PAIR * pair + n
                multiply_and_add_bias(i, j, range(BANKS_PER_ROW))
                if n == PAIR - 1 and True:
                    square_sum_on_vector(i, j, sums[:, n : n + 1])
                else:
                    square_sum(i, j, slice(0, HEADS), sums[:, n : n + 1])
            nc.scalar.activation(
                out=excess[:], in_=sums[:], func=ACT.Relu, bias=-NORM_FLOOR_SQUARED
            )
            return invert_norms(excess)

        def scale_mixed(i, pair, inverse, how):
            for word in how.split():
                n, who = int(word[0]), word[2]
                heads = slice(0, HEADS) if word[1] == "*" else head_groups[int(word[1])] if word[1] in "01" else slice(2 * "abcd".index(word[1]), 2 * "abcd".index(word[1]) + 2)
                y = y_all[:, i, heads, PAIR * pair + n, :]
                factor = inverse[:, n : n + 1]
                if who == "G":
                    nc.gpsimd.tensor_scalar(out=y, in0=y, scalar1=factor, scalar2=0.0, op0=ALU.mult, op1=ALU.add)
                elif who == "S":
                    nc.scalar.activation(out=y, in_=y, func=ACT.Copy, scale=factor)
                else:
                    nc.vector.tensor_scalar(out=y, in0=y, scalar1=factor, scalar2=None, op0=ALU.mult)

        def store(i, pair, groups=head_groups):
            tiles = slice(PAIR * pair, PAIR * (pair + 1))
            for heads in groups:
                nc.sync.dma_start(
                    out=projections[i]["out"][pair][heads].rearrange("h (c j) d -> c h (j d)", j=PAIR),
                    in_=y_all[:, i, heads, tiles, :].rearrange("p h j d -> p h (j d)"),
                )

        for j in range(PAIR):
            for g in range(PASSES):
                turn_x(j, [g], nc.scalar.copy)
                quantise_x(j, [g])
        spread_bias(Q, nc.scalar.copy)
        inverse = multiply_pair(Q, 0)
        both = list(range(PASSES))
        for j in range(PAIR, TOKEN_TILES):
            turn_x(j, both, nc.vector.tensor_copy)
        for j in range(PAIR, TOKEN_TILES):
            quantise_x(j, both)
        spread_bias(V, nc.vector.tensor_copy)
        scale_mixed(Q, 0, inverse, "00G 10S 01G 11S")
        multiply_and_add_bias(V, 0, [0])
        multiply_and_add_bias(V, 1, [0])
        multiply_and_add_bias(V, 2, [0])
        multiply_then_add_bias(V, 3, 0)
        spread_bias(K, nc.scalar.copy)
        scale_mixed(Q, 1, multiply_pair(Q, 1), "0*G 10G 11G")
        multiply_and_add_bias(V, 0, [1])
        multiply_and_add_bias(V, 1, [1])
        multiply_and_add_bias(V, 2, [1])
        multiply_and_add_bias(V, 3, [1])
        scale_mixed(K, 0, multiply_pair(K, 0), "00G 10S 01G 11S")
        scale_mixed(K, 1, multiply_last_pair(K, 1), "0aV 1aS 0bV 1bS 01V 11S")

        store(Q, 0)
        store(V, 0, [head_groups[0]])
        store(V, 1, [head_groups[0]])
        store(V, 0, [head_groups[1]])
        store(V, 1, [head_groups[1]])
        store(Q, 1)
        store(K, 0)
        store(K, 1, [slice(0, 2), slice(2, 4), head_groups[1]])
